import numpy as np
import ml_dtypes


def mxq(x, axis, fmt="e4m3"):
    dtype, down = {"e4m3": (ml_dtypes.float8_e4m3fn, 7), "e5m2": (ml_dtypes.float8_e5m2, 14)}[fmt]
    v = np.moveaxis(np.asarray(x, np.float32).astype(ml_dtypes.bfloat16).astype(np.float64), axis, -1)
    blocks = v.reshape(v.shape[:-1] + (-1, 32))
    amax = np.abs(blocks).max(-1, keepdims=True)
    byte = np.maximum(np.where(amax > 0, np.frexp(amax)[1] - 1 + 127, 0) - down, 1)
    scale = np.exp2(byte - 127.0)
    codes = (blocks / scale).astype(np.float32).astype(dtype).astype(np.float64)
    return np.moveaxis((codes * scale).reshape(v.shape), -1, axis)


WIDE = False


def mx_kscale(k):
    if not WIDE:
        return np.ones(k)
    levels = np.array([10, -10, 5, -5, 0])
    if k % 512:
        return np.exp2(np.random.permutation(np.resize(levels, k // 32))).repeat(32)
    a = np.empty((k // 512, 16))
    for p in range(k // 512):
        a[p, :8] = np.random.permutation(np.resize(levels, 8))
        for g in range(8):
            far = levels[np.abs(levels - a[p, g]) >= 10]
            a[p, g + 8] = far[np.random.randint(len(far))]
    return np.exp2(a.ravel()).repeat(32)


BF16 = ml_dtypes.bfloat16


def bf(x):
    return np.asarray(x, np.float32).astype(BF16)


def f64(x):
    return np.asarray(x).astype(np.float64)


E2M1 = np.array([0.0, 0.5, 1.0, 1.5, 2.0, 3.0, 4.0, 6.0, -0.0, -0.5, -1.0, -1.5, -2.0, -3.0, -4.0, -6.0])


def pack_weight(w, fmt):
    k, n = w.shape
    w = f64(bf(w)).reshape(k // 32, 32, n)
    amax = np.abs(w).max(1)
    if fmt == "e4m3":
        byte = np.frexp(amax)[1] - 1 + 127 - 7
    else:
        mant, ex = np.frexp(amax / 6.0)
        byte = np.where(mant > 0.5, ex, ex - 1) + 127
    byte = np.clip(np.where(amax > 0, byte, 1), 1, 254)
    scaled = (w * np.exp2(127.0 - byte)[:, None, :]).reshape(k, n).astype(np.float32)
    by_word = np.ascontiguousarray(scaled.reshape(k // 512, 128, 4, n).transpose(0, 1, 3, 2))
    if fmt == "e4m3":
        words = by_word.astype(ml_dtypes.float8_e4m3fn).view(np.uint8)
    else:
        c = by_word.astype(ml_dtypes.float4_e2m1fn).view(np.uint8) & 0xF
        words = c[..., 0::2] | (c[..., 1::2] << 4)
    return np.ascontiguousarray(words), np.ascontiguousarray(byte.astype(np.uint8).reshape(k // 512, 16, n))


def unpack_weight(words, scales, fmt):
    g, p, n, _ = words.shape
    if fmt == "e4m3":
        vals = np.ascontiguousarray(words).view(ml_dtypes.float8_e4m3fn).astype(np.float64)
    else:
        nib = np.empty((g, p, n, 4), np.uint8)
        nib[..., 0::2] = words & 0xF
        nib[..., 1::2] = words >> 4
        vals = E2M1[nib]
    vals = vals * np.repeat(np.exp2(scales.astype(np.float64) - 127.0), 8, axis=1)[..., None]
    return vals.transpose(0, 1, 3, 2).reshape(g * 512, n)
def pack4(w):
    words, scales = pack_weight(w, "e2m1")
    return words.reshape(words.shape[0], 128, -1), scales


def unpack4(words, scales):
    return unpack_weight(words.reshape(words.shape[0], 128, -1, 2), scales, "e2m1")


B, N, D, H = 128, 17, 2048, 32
D2 = D // 2
D4 = D // 4
EPS = 1e-5


def layernorm(z, g, b):
    mu = z.mean(-1, keepdims=True)
    var = z.var(-1, keepdims=True)
    return (z - mu) / np.sqrt(var + EPS) * g + b


def draw0():
    s, t = mx_kscale(D), mx_kscale(D2)
    r = np.random.standard_normal
    query = bf(r((B, N, D)) * s)
    A1W_words, A1W_scales = pack4(r((D, D2)) / np.sqrt(D) / s[:, None])
    A1b = bf(r(D2) * 0.2)
    g1 = bf((1.0 + 0.1 * r(D2)) * t)
    b1 = bf(r(D2) * 0.2 * t)
    A2W_words, A2W_scales = pack4(r((D2, D4)) / np.sqrt(D2) / t[:, None])
    return {"query": query,
            "A1W_words": A1W_words,
            "A1W_scales": A1W_scales,
            "A1b": A1b,
            "g1": g1,
            "b1": b1,
            "A2W_words": A2W_words,
            "A2W_scales": A2W_scales,
            "A2b": bf(r(D4) * 0.2),
            "g2": bf(1.0 + 0.1 * r(D4)),
            "b2": bf(r(D4) * 0.2)}


def core(query, A1W_words, A1W_scales, A1b, g1, b1, A2W_words, A2W_scales, A2b, g2, b2):
    u = (mxq(f64(query), 2, "e4m3") @ unpack4(A1W_words, A1W_scales)) + f64(A1b)
    j1 = np.maximum(layernorm(u, f64(g1), f64(b1)), 0.0)
    w = (mxq(j1, 2, "e4m3") @ unpack4(A2W_words, A2W_scales)) + f64(A2b)
    return np.maximum(layernorm(w, f64(g2), f64(b2)), 0.0)


def e4m3fn_bytes(y):
    return np.clip(np.asarray(y, np.float64), -448.0, 448.0).astype(np.float32).astype(ml_dtypes.float8_e4m3fn).view(np.uint8)


def e4m3fn_values(b):
    return np.asarray(b, np.uint8).view(ml_dtypes.float8_e4m3fn).astype(np.float64)


def setup_inputs():
    d = draw0()
    x0 = np.asarray(d['query']).astype(np.float64)
    s = (np.max(np.abs(x0), axis=(0, 1), keepdims=True) / 448.0).astype(np.float32)
    out = {}
    for k, v in d.items():
        if k == 'query':
            out['query_bytes'] = e4m3fn_bytes(x0 / s.astype(np.float64))
            out['query_scale'] = s
        else:
            out[k] = v
    return out


def reference(query_bytes, query_scale, A1W_words, A1W_scales, A1b, g1, b1, A2W_words, A2W_scales, A2b, g2, b2):
    return core(e4m3fn_values(query_bytes) * query_scale.astype(np.float64), A1W_words, A1W_scales, A1b, g1, b1, A2W_words, A2W_scales, A2b, g2, b2)

@@ -1,0 +1,312 @@
+from contextlib import ExitStack
+
+import concourse.mybir as mybir
+from concourse.masks import make_identity
+
+TOKENS, D, D2, D4 = 2176, 2048, 1024, 512
+P = 128
+PACK = 4
+K_PASS = P * PACK
+N_TILES = TOKENS // P
+PASSES1 = D // K_PASS
+PASSES2 = D2 // K_PASS
+HALF = 512
+EPS = 1e-5
+HUGE = 3.0e38
+
+FLOPS = 2 * TOKENS * (D * D2 + D2 * D4)
+
+F32 = mybir.dt.float32
+BF16 = mybir.dt.bfloat16
+I32 = mybir.dt.int32
+U32 = mybir.dt.uint32
+U8 = mybir.dt.uint8
+F8 = mybir.dt.float8_e4m3fn
+FP8X4 = mybir.dt.float8_e4m3fn_x4
+FP4X4 = mybir.dt.float4_e2m1fn_x4
+ACT = mybir.ActivationFunctionType
+ALU = mybir.AluOpType
+
+
+def tile_multiheadedattention_pa_w4_kernel(
+    tc, query_bytes, query_scale, A1W_words, A1W_scales, A1b, g1, b1, A2W_words, A2W_scales, A2b, g2, b2, out
+):
+    nc = tc.nc
+    x_hbm = query_bytes.rearrange("b n k -> (b n) k").rearrange("(i p) k -> p i k", p=P)
+    out_hbm = out.rearrange("b n c -> (b n) c").rearrange("(i p) c -> p i c", p=P)
+    scale_hbm = query_scale.rearrange("a b k -> (a b k)")
+
+    with ExitStack() as ctx:
+        keep = ctx.enter_context(tc.tile_pool(name="keep", bufs=1))
+        work = ctx.enter_context(tc.tile_pool(name="work", bufs=3))
+        small = ctx.enter_context(tc.tile_pool(name="small", bufs=4))
+        psum = ctx.enter_context(tc.psum_pool(name="psum", bufs=2))
+        ctx.enter_context(tc.manual_schedule())
+
+        x_bytes = keep.tile([P, N_TILES, D], U8, align_bytes=64)
+        x_scale = keep.tile([P, PASSES1, 1, 2, 2], F32, align_bytes=64)
+        w1 = keep.tile([P, PASSES1, 2 * D2], U8, align_bytes=64)
+        w1_scales = keep.tile([P, PASSES1, D2], U8, align_bytes=64)
+        w2 = keep.tile([P, PASSES2, 2 * D4], U8, align_bytes=64)
+        w2_scales = keep.tile([P, PASSES2, D4], U8, align_bytes=64)
+        bias1 = keep.tile([P, D2], BF16, align_bytes=64)
+        bias2 = keep.tile([P, D4], BF16, align_bytes=64)
+        gain2 = keep.tile([P, D4], BF16, align_bytes=64)
+        shift2 = keep.tile([P, D4], BF16, align_bytes=64)
+        gain1_raw = keep.tile([P, PASSES2, PACK], BF16)
+        shift1_raw = keep.tile([P, PASSES2, PACK], BF16)
+        gain1 = keep.tile([P, PASSES2, PACK], F32)
+        shift1 = keep.tile([P, PASSES2, PACK], F32)
+        minus_half = keep.tile([P, 1], F32)
+        warm = keep.tile([P, 1], F32)
+        warm_out = keep.tile([P, 1], F32)
+        ident = keep.tile([P, P], F32, align_bytes=64)
+
+        nc.vector.memset(warm[:], 0.0)
+        nc.vector.memset(w1_scales[:].rearrange("p g n -> p (g n)").bitcast(I32), 0)
+        nc.vector.memset(w2_scales[:].rearrange("p g n -> p (g n)").bitcast(I32), 0)
+        nc.gpsimd.memset(minus_half[:], -0.5)
+        make_identity(nc, ident[:])
+
+        nc.sync.dma_start(out=x_bytes[:, 0, :], in_=x_hbm[:, 0, :])
+        nc.scalar.dma_start(
+            out=x_scale[:].rearrange("p g o u e -> p g (o u e)"), in_=scale_hbm.rearrange("(g p t) -> p g t", p=P, t=PACK)
+        )
+        nc.scalar.activation(out=warm_out[:], in_=warm[:], func=ACT.Square)
+        for q in range(4):
+            nc.sync.dma_start(
+                out=w1_scales[32 * q : 32 * q + 4, :, :].bitcast(I32),
+                in_=A1W_scales[:, 4 * q : 4 * q + 4, :].rearrange("g q n -> q g n").bitcast(I32),
+            )
+        for q in range(4):
+            nc.sync.dma_start(
+                out=w2_scales[32 * q : 32 * q + 4, :, :].bitcast(I32),
+                in_=A2W_scales[:, 4 * q : 4 * q + 4, :].rearrange("g q n -> q g n").bitcast(I32),
+            )
+        for g in range(PASSES1):
+            nc.sync.dma_start(out=w1[:, g, :], in_=A1W_words[g])
+        nc.sync.dma_start(out=x_bytes[:, 1, :], in_=x_hbm[:, 1, :])
+        nc.sync.dma_start(out=x_bytes[:, 2:4, :], in_=x_hbm[:, 2:4, :])
+        nc.scalar.dma_start(out=bias1[:], in_=A1b.partition_broadcast(P))
+        nc.scalar.dma_start(out=gain1_raw[:], in_=g1.rearrange("(g p t) -> p g t", p=P, t=PACK))
+        nc.scalar.dma_start(out=shift1_raw[:], in_=b1.rearrange("(g p t) -> p g t", p=P, t=PACK))
+        for g in range(PASSES2):
+            nc.sync.dma_start(out=w2[:, g, :], in_=A2W_words[g])
+        nc.scalar.dma_start(out=bias2[:], in_=A2b.partition_broadcast(P))
+        nc.scalar.dma_start(out=gain2[:], in_=g2.partition_broadcast(P))
+        nc.scalar.dma_start(out=shift2[:], in_=b2.partition_broadcast(P))
+        for first, last in ((4, 8), (8, 12), (12, 17)):
+            nc.sync.dma_start(out=x_bytes[:, first:last, :], in_=x_hbm[:, first:last, :])
+        nc.gpsimd.tensor_copy(out=gain1[:], in_=gain1_raw[:])
+        nc.gpsimd.tensor_copy(out=shift1[:], in_=shift1_raw[:])
+
+        live = {}
+
+        def widen_x(i, h):
+            if h == 0:
+                live["xr", i] = work.tile([P, D], BF16, align_bytes=64, tag="xr", name="xr")
+            cols = slice(h * D // 2, (h + 1) * D // 2)
+            nc.scalar.copy(out=live["xr", i][:, cols], in_=x_bytes[:, i, cols].bitcast(F8))
+
+        def turn_x(i):
+            words = live.pop(("xr", i))[:].bitcast(F32)
+            xt = [psum.tile([P, 2, 2, P], F32, tag="xt", name="xt") for j in range(2)]
+            live["xt", i] = xt
+            for g in range(PASSES1):
+                for u in range(2):
+                    nc.tensor.transpose(xt[g // 2][:, g % 2, u, :], words[:, 256 * g + u : 256 * (g + 1) : 2], ident[:])
+
+        def scale_x(i):
+            xg = work.tile([P, PASSES1, P, PACK], BF16, align_bytes=64, tag="xg")
+            live["xg", i] = xg
+            xt = live.pop(("xt", i))
+            for g in range(PASSES1):
+                raw = xt[g // 2][:, g % 2].rearrange("p u r -> p (u r)").bitcast(BF16)
+                nc.vector.tensor_tensor(
+                    out=xg[:, g].rearrange("p r (u e) -> p r u e", u=2),
+                    in0=raw.rearrange("p (u r e) -> p r u e", u=2, e=2),
+                    in1=x_scale[:, g].to_broadcast([P, P, 2, 2]),
+                    op=ALU.mult,
+                )
+
+        def quantize_x(i):
+            xg = live.pop(("xg", i))
+            codes = work.tile([P, PASSES1 * P], U32, align_bytes=64, tag="xc")
+            scales = work.tile([P, PASSES1 * P], U8, align_bytes=64, tag="xsc")
+            live["xq", i] = (codes, scales)
+            nc.vector.quantize_mx(out=codes[:].bitcast(FP8X4), scales=scales[:], in_=xg[:].rearrange("p g r t -> p (g r t)"))
+
+        def layer1(i):
+            codes, scales = live.pop(("xq", i))
+            u = [psum.tile([P, HALF], F32, tag="u", name="u") for h in range(2)]
+            live["u", i] = u
+            for h in range(2):
+                for g in range(PASSES1):
+                    rows = slice(g * P, (g + 1) * P)
+                    nc.tensor.matmul_mx(
+                        out=u[h][:],
+                        lhsT=codes[:, rows].bitcast(FP8X4),
+                        lhsT_scale=scales[:, rows],
+                        rhs=w1[:, g, 2 * HALF * h : 2 * HALF * (h + 1)].bitcast(FP4X4),
+                        rhs_scale=w1_scales[:, g, HALF * h : HALF * (h + 1)],
+                        start=(g == 0),
+                        stop=(g == PASSES1 - 1),
+                    )
+
+        def bias_1(i):
+            v = work.tile([P, D2], F32, align_bytes=64, tag="v")
+            sums = small.tile([P, 2], F32, tag="sums")
+            live["v", i] = v
+            live["sums", i] = sums
+            for h, u in enumerate(live.pop(("u", i))):
+                cols = slice(HALF * h, HALF * (h + 1))
+                nc.vector.scalar_tensor_tensor(
+                    out=v[:, cols], in0=u[:], scalar=1.0, in1=bias1[:, cols], op0=ALU.mult, op1=ALU.add,
+                    accum_out=sums[:, h : h + 1],
+                )
+
+        def mean_1(i):
+            sums = live.pop(("sums", i))
+            nmean = small.tile([P, 1], F32, tag="nmean")
+            live["nmean", i] = nmean
+            nc.gpsimd.tensor_scalar(out=nmean[:], in0=sums[:, 0:1], scalar1=sums[:, 1:2], scalar2=-1.0 / D2, op0=ALU.add, op1=ALU.mult)
+
+        def square_1(i):
+            junk = work.tile([P, D2], BF16, align_bytes=64, tag="junk")
+            ssq = small.tile([P, 1], F32, tag="ssq")
+            live["ssq", i] = ssq
+            nc.scalar.activation(out=junk[:], in_=live["v", i][:], func=ACT.Square, bias=live["nmean", i][:], scale=1.0, accum_out=ssq[:])
+
+        def rstd(i, key, n):
+            ssq = live.pop((key, i))
+            var = small.tile([P, 1], F32, tag="var" + key)
+            r = small.tile([P, 1], F32, tag="r" + key)
+            nc.gpsimd.tensor_scalar(out=var[:], in0=ssq[:], scalar1=1.0 / n, scalar2=EPS, op0=ALU.mult, op1=ALU.add)
+            nc.gpsimd.tensor_tensor(out=r[:], in0=var[:], in1=minus_half[:], op=ALU.pow)
+            return r
+
+        def normalise_1(i):
+            r = rstd(i, "ssq", D2)
+            y = work.tile([P, PASSES2, PACK, P], F32, align_bytes=64, tag="y")
+            v = live.pop(("v", i))
+            nmean = live.pop(("nmean", i))
+            live["y", i] = y
+            nc.gpsimd.tensor_scalar(
+                out=y[:], in0=v[:].rearrange("p (g m t) -> p g t m", g=PASSES2, t=PACK), scalar1=nmean[:], scalar2=r[:],
+                op0=ALU.add, op1=ALU.mult,
+            )
+
+        def turn_y(i):
+            y = live.pop(("y", i))
+            yt = [psum.tile([P, PACK, P], F32, tag="yt", name="yt") for g in range(PASSES2)]
+            live["yt", i] = yt
+            for g in range(PASSES2):
+                for t in range(PACK):
+                    nc.tensor.transpose(yt[g][:, t, :], y[:, g, t, :], ident[:])
+
+        def relu_1(i):
+            jp = work.tile([P, PASSES2, PACK, P], BF16, align_bytes=64, tag="jp")
+            live["jp", i] = jp
+            for g, yt in enumerate(live.pop(("yt", i))):
+                for t in range(PACK):
+                    nc.scalar.activation(
+                        out=jp[:, g, t, :], in_=yt[:, t, :], func=ACT.Relu, bias=shift1[:, g, t : t + 1], scale=gain1[:, g, t : t + 1]
+                    )
+
+        def interleave_1(i):
+            jp = live.pop(("jp", i))
+            jg = work.tile([P, PASSES2, P, PACK], BF16, align_bytes=64, tag="jg")
+            live["jg", i] = jg
+            nc.gpsimd.tensor_scalar(
+                out=jg[:], in0=jp[:].rearrange("p g t r -> p g r t"), scalar1=1.0, scalar2=0.0, op0=ALU.mult, op1=ALU.add
+            )
+
+        def quantize_j(i):
+            jg = live.pop(("jg", i))
+            codes = work.tile([P, PASSES2 * P], U32, align_bytes=64, tag="jc")
+            scales = work.tile([P, PASSES2 * P], U8, align_bytes=64, tag="jsc")
+            live["jq", i] = (codes, scales)
+            nc.vector.quantize_mx(out=codes[:].bitcast(FP8X4), scales=scales[:], in_=jg[:].rearrange("p g r t -> p (g r t)"))
+
+        def layer2(i):
+            codes, scales = live.pop(("jq", i))
+            w = psum.tile([P, D4], F32, tag="w", bufs=1)
+            live["w", i] = w
+            for g in range(PASSES2):
+                rows = slice(g * P, (g + 1) * P)
+                nc.tensor.matmul_mx(
+                    out=w[:],
+                    lhsT=codes[:, rows].bitcast(FP8X4),
+                    lhsT_scale=scales[:, rows],
+                    rhs=w2[:, g, :].bitcast(FP4X4),
+                    rhs_scale=w2_scales[:, g, :],
+                    start=(g == 0),
+                    stop=(g == PASSES2 - 1),
+                )
+
+        def bias_2(i):
+            v = work.tile([P, D4], F32, align_bytes=64, tag="v2")
+            sums = small.tile([P, 1], F32, tag="sums2")
+            live["v2", i] = v
+            live["sums2", i] = sums
+            nc.vector.scalar_tensor_tensor(
+                out=v[:], in0=live.pop(("w", i))[:], scalar=1.0, in1=bias2[:], op0=ALU.mult, op1=ALU.add, accum_out=sums[:]
+            )
+
+        def mean_2(i):
+            sums = live.pop(("sums2", i))
+            nmean = small.tile([P, 1], F32, tag="nmean2")
+            live["nmean2", i] = nmean
+            nc.gpsimd.tensor_scalar(out=nmean[:], in0=sums[:], scalar1=-1.0 / D4, scalar2=0.0, op0=ALU.mult, op1=ALU.add)
+
+        def square_2(i):
+            junk = work.tile([P, D4], BF16, align_bytes=64, tag="junk2")
+            ssq = small.tile([P, 1], F32, tag="ssq2")
+            live["ssq2", i] = ssq
+            nc.scalar.activation(out=junk[:], in_=live["v2", i][:], func=ACT.Square, bias=live["nmean2", i][:], scale=1.0, accum_out=ssq[:])
+
+        def rstd_2(i):
+            live["r2", i] = rstd(i, "ssq2", D4)
+
+        def scale_2(i):
+            z = work.tile([P, D4], F32, align_bytes=64, tag="z")
+            o = work.tile([P, D4], F32, align_bytes=64, tag="o")
+            live["o", i] = o
+            v = live.pop(("v2", i))
+            nmean = live.pop(("nmean2", i))
+            r = live.pop(("r2", i))
+            nc.vector.scalar_tensor_tensor(out=z[:], in0=v[:], scalar=nmean[:], in1=gain2[:], op0=ALU.add, op1=ALU.mult)
+            nc.vector.scalar_tensor_tensor(out=o[:], in0=z[:], scalar=r[:], in1=shift2[:], op0=ALU.mult, op1=ALU.add)
+
+        def relu_2(i):
+            o = live.pop(("o", i))
+            res = work.tile([P, D4], F32, align_bytes=64, tag="res")
+            nc.gpsimd.tensor_scalar(out=res[:], in0=o[:], scalar1=HUGE, scalar2=0.0, op0=ALU.min, op1=ALU.max)
+            nc.sync.dma_start(out=out_hbm[:, i, :], in_=res[:])
+
+        def run(stage, i):
+            if 0 <= i < N_TILES:
+                stage(i)
+
+        for s in range(-3, N_TILES + 6):
+            run(turn_x, s + 1)
+            run(turn_y, s - 2)
+            run(relu_2, s - 5)
+            run(bias_1, s - 1)
+            run(mean_1, s - 1)
+            run(bias_2, s - 4)
+            run(mean_2, s - 4)
+            run(lambda i: widen_x(i, 0), s + 3)
+            run(square_1, s - 1)
+            run(square_2, s - 4)
+            run(normalise_1, s - 1)
+            run(rstd_2, s - 4)
+            run(scale_x, s + 1)
+            run(quantize_j, s - 3)
+            run(relu_1, s - 2)
+            run(interleave_1, s - 2)
+            run(lambda i: widen_x(i, 1), s + 3)
+            run(quantize_x, s + 1)
+            run(layer1, s)
+            run(layer2, s - 3)
+            run(scale_2, s - 4)

@@ -12,7 +12,6 @@ PASSES1 = D // K_PASS
 PASSES2 = D2 // K_PASS
 HALF = 512
 EPS = 1e-5
-HUGE = 3.0e38
 
 FLOPS = 2 * TOKENS * (D * D2 + D2 * D4)
 
@@ -27,6 +26,40 @@ FP4X4 = mybir.dt.float4_e2m1fn_x4
 ACT = mybir.ActivationFunctionType
 ALU = mybir.AluOpType
 
+ORDER = (
+    ("ex0", 2),
+    ("r2", 17),
+    ("o2", 18),
+    ("sq2", 15),
+    ("l0", 3),
+    ("ex1", 2),
+    ("qx", 2),
+    ("ty1", 5),
+    ("b0", 3),
+    ("m1", 4),
+    ("in0", 6),
+    ("ty0", 5),
+    ("l1", 3),
+    ("o1", 16),
+    ("sq", 4),
+    ("rl", 20),
+    ("tx0", 1),
+    ("re1", 5),
+    ("b1", 3),
+    ("r1", 4),
+    ("qj", 8),
+    ("l2", 10),
+    ("re0", 5),
+    ("c", 10),
+    ("y", 4),
+    ("m2", 14),
+    ("in1", 5),
+    ("st", 23),
+    ("tx1", 1),
+    ("TT", 0),
+)
+Y_ON_SCALAR = ()
+
 
 def tile_multiheadedattention_pa_w4_kernel(
     tc, query_bytes, query_scale, A1W_words, A1W_scales, A1b, g1, b1, A2W_words, A2W_scales, A2b, g2, b2, out
@@ -38,18 +71,19 @@ def tile_multiheadedattention_pa_w4_kernel(
 
     with ExitStack() as ctx:
         keep = ctx.enter_context(tc.tile_pool(name="keep", bufs=1))
-        work = ctx.enter_context(tc.tile_pool(name="work", bufs=3))
-        small = ctx.enter_context(tc.tile_pool(name="small", bufs=4))
+        work = ctx.enter_context(tc.tile_pool(name="work", bufs=4))
+        small = ctx.enter_context(tc.tile_pool(name="small", bufs=12))
         psum = ctx.enter_context(tc.psum_pool(name="psum", bufs=2))
         ctx.enter_context(tc.manual_schedule())
 
         x_bytes = keep.tile([P, N_TILES, D], U8, align_bytes=64)
-        x_scale = keep.tile([P, PASSES1, 1, 2, 2], F32, align_bytes=64)
+        x_scale = keep.tile([P, D], F32, align_bytes=64)
         w1 = keep.tile([P, PASSES1, 2 * D2], U8, align_bytes=64)
         w1_scales = keep.tile([P, PASSES1, D2], U8, align_bytes=64)
         w2 = keep.tile([P, PASSES2, 2 * D4], U8, align_bytes=64)
         w2_scales = keep.tile([P, PASSES2, D4], U8, align_bytes=64)
-        bias1 = keep.tile([P, D2], BF16, align_bytes=64)
+        bias1_raw = keep.tile([P, PASSES2, P, PACK], BF16, align_bytes=64)
+        bias1 = keep.tile([P, PASSES2, PACK, P], BF16, align_bytes=64)
         bias2 = keep.tile([P, D4], BF16, align_bytes=64)
         gain2 = keep.tile([P, D4], BF16, align_bytes=64)
         shift2 = keep.tile([P, D4], BF16, align_bytes=64)
@@ -57,22 +91,22 @@ def tile_multiheadedattention_pa_w4_kernel(
         shift1_raw = keep.tile([P, PASSES2, PACK], BF16)
         gain1 = keep.tile([P, PASSES2, PACK], F32)
         shift1 = keep.tile([P, PASSES2, PACK], F32)
-        minus_half = keep.tile([P, 1], F32)
-        warm = keep.tile([P, 1], F32)
+        eps = keep.tile([P, 1], F32)
         warm_out = keep.tile([P, 1], F32)
+        junk = keep.tile([P, 2], F32)
         ident = keep.tile([P, P], F32, align_bytes=64)
 
-        nc.vector.memset(warm[:], 0.0)
+        nc.vector.memset(eps[:], EPS)
         nc.vector.memset(w1_scales[:].rearrange("p g n -> p (g n)").bitcast(I32), 0)
         nc.vector.memset(w2_scales[:].rearrange("p g n -> p (g n)").bitcast(I32), 0)
-        nc.gpsimd.memset(minus_half[:], -0.5)
         make_identity(nc, ident[:])
 
         nc.sync.dma_start(out=x_bytes[:, 0, :], in_=x_hbm[:, 0, :])
-        nc.scalar.dma_start(
-            out=x_scale[:].rearrange("p g o u e -> p g (o u e)"), in_=scale_hbm.rearrange("(g p t) -> p g t", p=P, t=PACK)
-        )
-        nc.scalar.activation(out=warm_out[:], in_=warm[:], func=ACT.Square)
+        for g in range(PASSES1):
+            cols = slice(g * K_PASS, (g + 1) * K_PASS)
+            nc.scalar.dma_start(out=x_scale[:, cols], in_=scale_hbm[cols].partition_broadcast(P))
+        nc.scalar.activation(out=warm_out[:], in_=eps[:], func=ACT.Abs_reciprocal_sqrt)
+        nc.sync.dma_start(out=x_bytes[:, 1, :], in_=x_hbm[:, 1, :])
         for q in range(4):
             nc.sync.dma_start(
                 out=w1_scales[32 * q : 32 * q + 4, :, :].bitcast(I32),
@@ -85,9 +119,8 @@ def tile_multiheadedattention_pa_w4_kernel(
             )
         for g in range(PASSES1):
             nc.sync.dma_start(out=w1[:, g, :], in_=A1W_words[g])
-        nc.sync.dma_start(out=x_bytes[:, 1, :], in_=x_hbm[:, 1, :])
         nc.sync.dma_start(out=x_bytes[:, 2:4, :], in_=x_hbm[:, 2:4, :])
-        nc.scalar.dma_start(out=bias1[:], in_=A1b.partition_broadcast(P))
+        nc.scalar.dma_start(out=bias1_raw[:].rearrange("p g m t -> p (g m t)"), in_=A1b.partition_broadcast(P))
         nc.scalar.dma_start(out=gain1_raw[:], in_=g1.rearrange("(g p t) -> p g t", p=P, t=PACK))
         nc.scalar.dma_start(out=shift1_raw[:], in_=b1.rearrange("(g p t) -> p g t", p=P, t=PACK))
         for g in range(PASSES2):
@@ -97,138 +130,136 @@ def tile_multiheadedattention_pa_w4_kernel(
         nc.scalar.dma_start(out=shift2[:], in_=b2.partition_broadcast(P))
         for first, last in ((4, 8), (8, 12), (12, 17)):
             nc.sync.dma_start(out=x_bytes[:, first:last, :], in_=x_hbm[:, first:last, :])
-        nc.gpsimd.tensor_copy(out=gain1[:], in_=gain1_raw[:])
-        nc.gpsimd.tensor_copy(out=shift1[:], in_=shift1_raw[:])
 
         live = {}
 
-        def widen_x(i, h):
-            if h == 0:
-                live["xr", i] = work.tile([P, D], BF16, align_bytes=64, tag="xr", name="xr")
-            cols = slice(h * D // 2, (h + 1) * D // 2)
-            nc.scalar.copy(out=live["xr", i][:, cols], in_=x_bytes[:, i, cols].bitcast(F8))
-
-        def turn_x(i):
-            words = live.pop(("xr", i))[:].bitcast(F32)
-            xt = [psum.tile([P, 2, 2, P], F32, tag="xt", name="xt") for j in range(2)]
-            live["xt", i] = xt
-            for g in range(PASSES1):
-                for u in range(2):
-                    nc.tensor.transpose(xt[g // 2][:, g % 2, u, :], words[:, 256 * g + u : 256 * (g + 1) : 2], ident[:])
-
-        def scale_x(i):
-            xg = work.tile([P, PASSES1, P, PACK], BF16, align_bytes=64, tag="xg")
-            live["xg", i] = xg
-            xt = live.pop(("xt", i))
-            for g in range(PASSES1):
-                raw = xt[g // 2][:, g % 2].rearrange("p u r -> p (u r)").bitcast(BF16)
+        def stage_TT(i):
+            xs = work.tile([P, D], BF16, align_bytes=64, tag="xs")
+            live["xs", i] = xs
+            step = D if i else HALF
+            for c in range(0, D, step):
                 nc.vector.tensor_tensor(
-                    out=xg[:, g].rearrange("p r (u e) -> p r u e", u=2),
-                    in0=raw.rearrange("p (u r e) -> p r u e", u=2, e=2),
-                    in1=x_scale[:, g].to_broadcast([P, P, 2, 2]),
+                    out=xs[:, c : c + step],
+                    in0=x_bytes[:, i, c : c + step].bitcast(F8),
+                    in1=x_scale[:, c : c + step],
                     op=ALU.mult,
                 )
 
-        def quantize_x(i):
+        def turn_x(i, h):
+            words = live["xs", i][:].bitcast(F32)
+            xt = psum.tile([P, 2, 2, P], F32, tag="xt")
+            live["xt", i, h] = xt
+            for g in range(2):
+                for u in range(2):
+                    first = 256 * (2 * h + g) + u
+                    nc.tensor.transpose(xt[:, g, u, :], words[:, first : first - u + 256 : 2], ident[:])
+
+        def empty_x(i, h):
+            if ("xg", i) not in live:
+                live["xg", i] = work.tile([P, PASSES1, P, PACK], BF16, align_bytes=64, tag="xg", name="xg")
+            words = live["xg", i][:].rearrange("p g r t -> p (g r t)").bitcast(F32).rearrange("p (g r u) -> p g r u", g=PASSES1, u=2)
+            nc.scalar.copy(out=words[:, 2 * h : 2 * h + 2], in_=live.pop(("xt", i, h))[:].rearrange("p g u r -> p g r u"))
+
+        def stage_qx(i):
             xg = live.pop(("xg", i))
             codes = work.tile([P, PASSES1 * P], U32, align_bytes=64, tag="xc")
             scales = work.tile([P, PASSES1 * P], U8, align_bytes=64, tag="xsc")
             live["xq", i] = (codes, scales)
             nc.vector.quantize_mx(out=codes[:].bitcast(FP8X4), scales=scales[:], in_=xg[:].rearrange("p g r t -> p (g r t)"))
 
-        def layer1(i):
-            codes, scales = live.pop(("xq", i))
-            u = [psum.tile([P, HALF], F32, tag="u", name="u") for h in range(2)]
-            live["u", i] = u
-            for h in range(2):
-                for g in range(PASSES1):
-                    rows = slice(g * P, (g + 1) * P)
-                    nc.tensor.matmul_mx(
-                        out=u[h][:],
-                        lhsT=codes[:, rows].bitcast(FP8X4),
-                        lhsT_scale=scales[:, rows],
-                        rhs=w1[:, g, 2 * HALF * h : 2 * HALF * (h + 1)].bitcast(FP4X4),
-                        rhs_scale=w1_scales[:, g, HALF * h : HALF * (h + 1)],
-                        start=(g == 0),
-                        stop=(g == PASSES1 - 1),
-                    )
-
-        def bias_1(i):
-            v = work.tile([P, D2], F32, align_bytes=64, tag="v")
-            sums = small.tile([P, 2], F32, tag="sums")
-            live["v", i] = v
-            live["sums", i] = sums
-            for h, u in enumerate(live.pop(("u", i))):
-                cols = slice(HALF * h, HALF * (h + 1))
-                nc.vector.scalar_tensor_tensor(
-                    out=v[:, cols], in0=u[:], scalar=1.0, in1=bias1[:, cols], op0=ALU.mult, op1=ALU.add,
-                    accum_out=sums[:, h : h + 1],
+        def layer1(i, h):
+            codes, scales = live["xq", i]
+            u = psum.tile([P, HALF], F32, tag="u")
+            live["u", i, h] = u
+            for g in range(PASSES1):
+                rows = slice(g * P, (g + 1) * P)
+                nc.tensor.matmul_mx(
+                    out=u[:],
+                    lhsT=codes[:, rows].bitcast(FP8X4),
+                    lhsT_scale=scales[:, rows],
+                    rhs=w1[:, g, 2 * HALF * h : 2 * HALF * (h + 1)].bitcast(FP4X4),
+                    rhs_scale=w1_scales[:, g, HALF * h : HALF * (h + 1)],
+                    start=(g == 0),
+                    stop=(g == PASSES1 - 1),
                 )
 
-        def mean_1(i):
-            sums = live.pop(("sums", i))
+        def bias_1(i, h):
+            if ("v", i) not in live:
+                live["v", i] = work.tile([P, PASSES2, PACK, P], F32, align_bytes=64, tag="v", name="v")
+                live["sums", i] = small.tile([P, 2], F32, tag="sums", name="sums")
+            nc.vector.scalar_tensor_tensor(
+                out=live["v", i][:, h],
+                in0=live.pop(("u", i, h))[:].rearrange("p (m t) -> p t m", t=PACK),
+                scalar=1.0,
+                in1=bias1[:, h],
+                op0=ALU.mult,
+                op1=ALU.add,
+                accum_out=live["sums", i][:, h : h + 1],
+            )
+
+        def stage_m1(i):
             nmean = small.tile([P, 1], F32, tag="nmean")
             live["nmean", i] = nmean
-            nc.gpsimd.tensor_scalar(out=nmean[:], in0=sums[:, 0:1], scalar1=sums[:, 1:2], scalar2=-1.0 / D2, op0=ALU.add, op1=ALU.mult)
+            nc.scalar.activation(out=junk[:], in_=live.pop(("sums", i))[:], func=ACT.Copy, scale=-1.0 / D2, accum_out=nmean[:])
 
-        def square_1(i):
-            junk = work.tile([P, D2], BF16, align_bytes=64, tag="junk")
+        def stage_sq(i):
+            waste = work.tile([P, D2], BF16, align_bytes=64, tag="waste", bufs=2)
             ssq = small.tile([P, 1], F32, tag="ssq")
             live["ssq", i] = ssq
-            nc.scalar.activation(out=junk[:], in_=live["v", i][:], func=ACT.Square, bias=live["nmean", i][:], scale=1.0, accum_out=ssq[:])
+            nc.scalar.activation(
+                out=waste[:], in_=live["v", i][:].rearrange("p g t m -> p (g t m)"), func=ACT.Square, bias=live["nmean", i][:],
+                scale=1.0, accum_out=ssq[:],
+            )
 
-        def rstd(i, key, n):
-            ssq = live.pop((key, i))
-            var = small.tile([P, 1], F32, tag="var" + key)
-            r = small.tile([P, 1], F32, tag="r" + key)
-            nc.gpsimd.tensor_scalar(out=var[:], in0=ssq[:], scalar1=1.0 / n, scalar2=EPS, op0=ALU.mult, op1=ALU.add)
-            nc.gpsimd.tensor_tensor(out=r[:], in0=var[:], in1=minus_half[:], op=ALU.pow)
-            return r
+        def stage_r1(i):
+            r = small.tile([P, 1], F32, tag="r1")
+            live["r1", i] = r
+            nc.scalar.activation(out=r[:], in_=live.pop(("ssq", i))[:], func=ACT.Abs_reciprocal_sqrt, bias=eps[:], scale=1.0 / D2)
+            if i in Y_ON_SCALAR:
+                nmr = small.tile([P, 1], F32, tag="nmr")
+                live["nmr", i] = nmr
+                nc.scalar.activation(out=nmr[:], in_=live["nmean", i][:], func=ACT.Copy, scale=r[:])
 
-        def normalise_1(i):
-            r = rstd(i, "ssq", D2)
+        def stage_y(i):
             y = work.tile([P, PASSES2, PACK, P], F32, align_bytes=64, tag="y")
-            v = live.pop(("v", i))
-            nmean = live.pop(("nmean", i))
             live["y", i] = y
-            nc.gpsimd.tensor_scalar(
-                out=y[:], in0=v[:].rearrange("p (g m t) -> p g t m", g=PASSES2, t=PACK), scalar1=nmean[:], scalar2=r[:],
-                op0=ALU.add, op1=ALU.mult,
-            )
+            v = live.pop(("v", i))
+            r = live.pop(("r1", i))
+            nmean = live.pop(("nmean", i))
+            if i in Y_ON_SCALAR:
+                nc.scalar.activation(out=y[:], in_=v[:], func=ACT.Identity, bias=live.pop(("nmr", i))[:], scale=r[:])
+            else:
+                nc.vector.tensor_scalar(out=y[:], in0=v[:], scalar1=nmean[:], scalar2=r[:], op0=ALU.add, op1=ALU.mult)
 
-        def turn_y(i):
-            y = live.pop(("y", i))
-            yt = [psum.tile([P, PACK, P], F32, tag="yt", name="yt") for g in range(PASSES2)]
-            live["yt", i] = yt
-            for g in range(PASSES2):
-                for t in range(PACK):
-                    nc.tensor.transpose(yt[g][:, t, :], y[:, g, t, :], ident[:])
+        def turn_y(i, g):
+            yt = psum.tile([P, PACK, P], F32, tag="yt")
+            live["yt", i, g] = yt
+            for t in range(PACK):
+                nc.tensor.transpose(yt[:, t, :], live["y", i][:, g, t, :], ident[:])
 
-        def relu_1(i):
-            jp = work.tile([P, PASSES2, PACK, P], BF16, align_bytes=64, tag="jp")
-            live["jp", i] = jp
-            for g, yt in enumerate(live.pop(("yt", i))):
-                for t in range(PACK):
-                    nc.scalar.activation(
-                        out=jp[:, g, t, :], in_=yt[:, t, :], func=ACT.Relu, bias=shift1[:, g, t : t + 1], scale=gain1[:, g, t : t + 1]
-                    )
+        def relu_1(i, g):
+            if ("jp", i) not in live:
+                live["jp", i] = work.tile([P, PASSES2, PACK, P], BF16, align_bytes=64, tag="jp", name="jp")
+            yt = live.pop(("yt", i, g))
+            for t in range(PACK):
+                nc.scalar.activation(
+                    out=live["jp", i][:, g, t, :], in_=yt[:, t, :], func=ACT.Relu, bias=shift1[:, g, t : t + 1],
+                    scale=gain1[:, g, t : t + 1],
+                )
 
-        def interleave_1(i):
-            jp = live.pop(("jp", i))
-            jg = work.tile([P, PASSES2, P, PACK], BF16, align_bytes=64, tag="jg")
-            live["jg", i] = jg
-            nc.gpsimd.tensor_scalar(
-                out=jg[:], in0=jp[:].rearrange("p g t r -> p g r t"), scalar1=1.0, scalar2=0.0, op0=ALU.mult, op1=ALU.add
-            )
+        def interleave(i, g):
+            if ("jg", i) not in live:
+                live["jg", i] = work.tile([P, PASSES2, P, PACK], BF16, align_bytes=64, tag="jg", name="jg")
+            nc.scalar.copy(out=live["jg", i][:, g], in_=live["jp", i][:, g].rearrange("p t r -> p r t"))
 
-        def quantize_j(i):
+        def stage_qj(i):
             jg = live.pop(("jg", i))
             codes = work.tile([P, PASSES2 * P], U32, align_bytes=64, tag="jc")
             scales = work.tile([P, PASSES2 * P], U8, align_bytes=64, tag="jsc")
             live["jq", i] = (codes, scales)
             nc.vector.quantize_mx(out=codes[:].bitcast(FP8X4), scales=scales[:], in_=jg[:].rearrange("p g r t -> p (g r t)"))
 
-        def layer2(i):
+        def stage_l2(i):
             codes, scales = live.pop(("jq", i))
             w = psum.tile([P, D4], F32, tag="w", bufs=1)
             live["w", i] = w
@@ -244,8 +275,8 @@ def tile_multiheadedattention_pa_w4_kernel(
                     stop=(g == PASSES2 - 1),
                 )
 
-        def bias_2(i):
-            v = work.tile([P, D4], F32, align_bytes=64, tag="v2")
+        def stage_c(i):
+            v = work.tile([P, D4], F32, align_bytes=64, tag="v2", bufs=10)
             sums = small.tile([P, 1], F32, tag="sums2")
             live["v2", i] = v
             live["sums2", i] = sums
@@ -253,60 +284,59 @@ def tile_multiheadedattention_pa_w4_kernel(
                 out=v[:], in0=live.pop(("w", i))[:], scalar=1.0, in1=bias2[:], op0=ALU.mult, op1=ALU.add, accum_out=sums[:]
             )
 
-        def mean_2(i):
-            sums = live.pop(("sums2", i))
+        def stage_m2(i):
             nmean = small.tile([P, 1], F32, tag="nmean2")
             live["nmean2", i] = nmean
-            nc.gpsimd.tensor_scalar(out=nmean[:], in0=sums[:], scalar1=-1.0 / D4, scalar2=0.0, op0=ALU.mult, op1=ALU.add)
+            nc.scalar.activation(out=nmean[:], in_=live.pop(("sums2", i))[:], func=ACT.Copy, scale=-1.0 / D4)
 
-        def square_2(i):
-            junk = work.tile([P, D4], BF16, align_bytes=64, tag="junk2")
+        def stage_sq2(i):
+            waste = work.tile([P, D4], BF16, align_bytes=64, tag="waste2", bufs=2)
             ssq = small.tile([P, 1], F32, tag="ssq2")
             live["ssq2", i] = ssq
-            nc.scalar.activation(out=junk[:], in_=live["v2", i][:], func=ACT.Square, bias=live["nmean2", i][:], scale=1.0, accum_out=ssq[:])
+            nc.scalar.activation(out=waste[:], in_=live["v2", i][:], func=ACT.Square, bias=live["nmean2", i][:], scale=1.0, accum_out=ssq[:])
 
-        def rstd_2(i):
-            live["r2", i] = rstd(i, "ssq2", D4)
+        def stage_r2(i):
+            r = small.tile([P, 1], F32, tag="r2")
+            live["r2", i] = r
+            nc.scalar.activation(out=r[:], in_=live.pop(("ssq2", i))[:], func=ACT.Abs_reciprocal_sqrt, bias=eps[:], scale=1.0 / D4)
 
-        def scale_2(i):
+        def stage_o1(i):
             z = work.tile([P, D4], F32, align_bytes=64, tag="z")
+            live["z", i] = z
+            nc.vector.scalar_tensor_tensor(
+                out=z[:], in0=live["v2", i][:], scalar=live["nmean2", i][:], in1=gain2[:], op0=ALU.add, op1=ALU.mult
+            )
+
+        def stage_o2(i):
             o = work.tile([P, D4], F32, align_bytes=64, tag="o")
             live["o", i] = o
-            v = live.pop(("v2", i))
-            nmean = live.pop(("nmean2", i))
-            r = live.pop(("r2", i))
-            nc.vector.scalar_tensor_tensor(out=z[:], in0=v[:], scalar=nmean[:], in1=gain2[:], op0=ALU.add, op1=ALU.mult)
-            nc.vector.scalar_tensor_tensor(out=o[:], in0=z[:], scalar=r[:], in1=shift2[:], op0=ALU.mult, op1=ALU.add)
+            nc.vector.scalar_tensor_tensor(
+                out=o[:], in0=live.pop(("z", i))[:], scalar=live.pop(("r2", i))[:], in1=shift2[:], op0=ALU.mult, op1=ALU.add
+            )
 
-        def relu_2(i):
+        def stage_rl(i):
             o = live.pop(("o", i))
             res = work.tile([P, D4], F32, align_bytes=64, tag="res")
-            nc.gpsimd.tensor_scalar(out=res[:], in0=o[:], scalar1=HUGE, scalar2=0.0, op0=ALU.min, op1=ALU.max)
-            nc.sync.dma_start(out=out_hbm[:, i, :], in_=res[:])
+            live["res", i] = res
+            nc.scalar.activation(out=res[:], in_=o[:], func=ACT.Relu)
 
-        def run(stage, i):
-            if 0 <= i < N_TILES:
-                stage(i)
+        def stage_st(i):
+            nc.sync.dma_start(out=out_hbm[:, i, :], in_=live.pop(("res", i))[:])
 
-        for s in range(-3, N_TILES + 6):
-            run(turn_x, s + 1)
-            run(turn_y, s - 2)
-            run(relu_2, s - 5)
-            run(bias_1, s - 1)
-            run(mean_1, s - 1)
-            run(bias_2, s - 4)
-            run(mean_2, s - 4)
-            run(lambda i: widen_x(i, 0), s + 3)
-            run(square_1, s - 1)
-            run(square_2, s - 4)
-            run(normalise_1, s - 1)
-            run(rstd_2, s - 4)
-            run(scale_x, s + 1)
-            run(quantize_j, s - 3)
-            run(relu_1, s - 2)
-            run(interleave_1, s - 2)
-            run(lambda i: widen_x(i, 1), s + 3)
-            run(quantize_x, s + 1)
-            run(layer1, s)
-            run(layer2, s - 3)
-            run(scale_2, s - 4)
+        stages = {
+            "TT": stage_TT, "tx0": lambda i: turn_x(i, 0), "tx1": lambda i: turn_x(i, 1), "ex0": lambda i: empty_x(i, 0),
+            "ex1": lambda i: empty_x(i, 1), "qx": stage_qx, "l0": lambda i: layer1(i, 0), "l1": lambda i: layer1(i, 1),
+            "b0": lambda i: bias_1(i, 0), "b1": lambda i: bias_1(i, 1), "m1": stage_m1, "sq": stage_sq, "r1": stage_r1, "y": stage_y,
+            "ty0": lambda i: turn_y(i, 0), "ty1": lambda i: turn_y(i, 1), "re0": lambda i: relu_1(i, 0), "re1": lambda i: relu_1(i, 1),
+            "in0": lambda i: interleave(i, 0), "in1": lambda i: interleave(i, 1), "qj": stage_qj, "l2": stage_l2, "c": stage_c,
+            "m2": stage_m2, "sq2": stage_sq2, "r2": stage_r2, "o1": stage_o1, "o2": stage_o2, "rl": stage_rl, "st": stage_st,
+        }
+        lags = [lag for name, lag in ORDER]
+        for step in range(min(lags), N_TILES + max(lags)):
+            for name, lag in ORDER:
+                if 0 <= step - lag < N_TILES:
+                    stages[name](step - lag)
+                    if name == "ex1" and step == lag:
+                        nc.scalar.copy(out=bias1[:], in_=bias1_raw[:].rearrange("p g m t -> p g t m"))
+                        nc.scalar.copy(out=gain1[:], in_=gain1_raw[:])
+                        nc.scalar.copy(out=shift1[:], in_=shift1_raw[:])

@@ -27,38 +27,37 @@ ACT = mybir.ActivationFunctionType
 ALU = mybir.AluOpType
 
 ORDER = (
-    ("ex0", 2),
-    ("r2", 17),
-    ("o2", 18),
-    ("sq2", 15),
-    ("l0", 3),
-    ("ex1", 2),
-    ("qx", 2),
-    ("ty1", 5),
-    ("b0", 3),
-    ("m1", 4),
-    ("in0", 6),
-    ("ty0", 5),
-    ("l1", 3),
-    ("o1", 16),
-    ("sq", 4),
-    ("rl", 20),
-    ("tx0", 1),
-    ("re1", 5),
-    ("b1", 3),
-    ("r1", 4),
-    ("qj", 8),
-    ("l2", 10),
-    ("re0", 5),
-    ("c", 10),
-    ("y", 4),
-    ("m2", 14),
-    ("in1", 5),
-    ("st", 23),
-    ("tx1", 1),
     ("TT", 0),
+    ("m1", 3),
+    ("in1", 5),
+    ("ty1", 4),
+    ("l2", 8),
+    ("qx", 1),
+    ("b1", 2),
+    ("b0", 2),
+    ("sq", 3),
+    ("tx0", 0),
+    ("re0", 4),
+    ("tx1", 0),
+    ("r2", 15),
+    ("qj", 7),
+    ("r1", 3),
+    ("in0", 4),
+    ("st", 22),
+    ("y", 3),
+    ("l1", 1),
+    ("o1", 14),
+    ("c", 8),
+    ("rl", 19),
+    ("ty0", 3),
+    ("re1", 4),
+    ("ex0", 0),
+    ("m2", 9),
+    ("l0", 1),
+    ("sq2", 11),
+    ("ex1", 0),
+    ("o2", 16),
 )
-Y_ON_SCALAR = ()
 
 
 def tile_multiheadedattention_pa_w4_kernel(
@@ -72,7 +71,7 @@ def tile_multiheadedattention_pa_w4_kernel(
     with ExitStack() as ctx:
         keep = ctx.enter_context(tc.tile_pool(name="keep", bufs=1))
         work = ctx.enter_context(tc.tile_pool(name="work", bufs=4))
-        small = ctx.enter_context(tc.tile_pool(name="small", bufs=12))
+        small = ctx.enter_context(tc.tile_pool(name="small", bufs=N_TILES))
         psum = ctx.enter_context(tc.psum_pool(name="psum", bufs=2))
         ctx.enter_context(tc.manual_schedule())
 
@@ -82,8 +81,7 @@ def tile_multiheadedattention_pa_w4_kernel(
         w1_scales = keep.tile([P, PASSES1, D2], U8, align_bytes=64)
         w2 = keep.tile([P, PASSES2, 2 * D4], U8, align_bytes=64)
         w2_scales = keep.tile([P, PASSES2, D4], U8, align_bytes=64)
-        bias1_raw = keep.tile([P, PASSES2, P, PACK], BF16, align_bytes=64)
-        bias1 = keep.tile([P, PASSES2, PACK, P], BF16, align_bytes=64)
+        bias1 = keep.tile([P, D2], BF16, align_bytes=64)
         bias2 = keep.tile([P, D4], BF16, align_bytes=64)
         gain2 = keep.tile([P, D4], BF16, align_bytes=64)
         shift2 = keep.tile([P, D4], BF16, align_bytes=64)
@@ -95,16 +93,17 @@ def tile_multiheadedattention_pa_w4_kernel(
         warm_out = keep.tile([P, 1], F32)
         junk = keep.tile([P, 2], F32)
         ident = keep.tile([P, P], F32, align_bytes=64)
+        scale_rows = keep.tile([P, P], F32, align_bytes=64)
+        scale_cols = keep.tile([P, D // P], F32, align_bytes=64)
 
+        nc.vector.memset(scale_rows[:], 0.0)
         nc.vector.memset(eps[:], EPS)
         nc.vector.memset(w1_scales[:].rearrange("p g n -> p (g n)").bitcast(I32), 0)
         nc.vector.memset(w2_scales[:].rearrange("p g n -> p (g n)").bitcast(I32), 0)
         make_identity(nc, ident[:])
 
         nc.sync.dma_start(out=x_bytes[:, 0, :], in_=x_hbm[:, 0, :])
-        for g in range(PASSES1):
-            cols = slice(g * K_PASS, (g + 1) * K_PASS)
-            nc.scalar.dma_start(out=x_scale[:, cols], in_=scale_hbm[cols].partition_broadcast(P))
+        nc.scalar.dma_start(out=scale_rows[: D // P, :], in_=scale_hbm.rearrange("(c n) -> c n", n=P))
         nc.scalar.activation(out=warm_out[:], in_=eps[:], func=ACT.Abs_reciprocal_sqrt)
         nc.sync.dma_start(out=x_bytes[:, 1, :], in_=x_hbm[:, 1, :])
         for q in range(4):
@@ -120,7 +119,7 @@ def tile_multiheadedattention_pa_w4_kernel(
         for g in range(PASSES1):
             nc.sync.dma_start(out=w1[:, g, :], in_=A1W_words[g])
         nc.sync.dma_start(out=x_bytes[:, 2:4, :], in_=x_hbm[:, 2:4, :])
-        nc.scalar.dma_start(out=bias1_raw[:].rearrange("p g m t -> p (g m t)"), in_=A1b.partition_broadcast(P))
+        nc.scalar.dma_start(out=bias1[:], in_=A1b.partition_broadcast(P))
         nc.scalar.dma_start(out=gain1_raw[:], in_=g1.rearrange("(g p t) -> p g t", p=P, t=PACK))
         nc.scalar.dma_start(out=shift1_raw[:], in_=b1.rearrange("(g p t) -> p g t", p=P, t=PACK))
         for g in range(PASSES2):
@@ -130,6 +129,18 @@ def tile_multiheadedattention_pa_w4_kernel(
         nc.scalar.dma_start(out=shift2[:], in_=b2.partition_broadcast(P))
         for first, last in ((4, 8), (8, 12), (12, 17)):
             nc.sync.dma_start(out=x_bytes[:, first:last, :], in_=x_hbm[:, first:last, :])
+        nc.gpsimd.tensor_copy(out=gain1[:], in_=gain1_raw[:])
+        nc.gpsimd.tensor_copy(out=shift1[:], in_=shift1_raw[:])
+
+        turned = psum.tile([P, P], F32, tag="w", bufs=1)
+        nc.tensor.transpose(turned[:], scale_rows[:], ident[:])
+        nc.vector.tensor_copy(out=scale_cols[:], in_=turned[:, : D // P])
+        for g in range(PASSES1):
+            spread = psum.tile([P, PACK, P], F32, tag=("xt", "yt")[g % 2])
+            for t in range(PACK):
+                nc.tensor.transpose(spread[:, t, :], scale_cols[:, PACK * g + t : PACK * g + t + 1].to_broadcast([P, P]), ident[:])
+            cols = slice(g * K_PASS, (g + 1) * K_PASS)
+            nc.scalar.copy(out=x_scale[:, cols], in_=spread[:].rearrange("p t n -> p (t n)"))
 
         live = {}
 
@@ -185,13 +196,13 @@ def tile_multiheadedattention_pa_w4_kernel(
 
         def bias_1(i, h):
             if ("v", i) not in live:
-                live["v", i] = work.tile([P, PASSES2, PACK, P], F32, align_bytes=64, tag="v", name="v")
+                live["v", i] = work.tile([P, D2], F32, align_bytes=64, tag="v", name="v")
                 live["sums", i] = small.tile([P, 2], F32, tag="sums", name="sums")
             nc.vector.scalar_tensor_tensor(
-                out=live["v", i][:, h],
-                in0=live.pop(("u", i, h))[:].rearrange("p (m t) -> p t m", t=PACK),
+                out=live["v", i][:, HALF * h : HALF * (h + 1)],
+                in0=live.pop(("u", i, h))[:],
                 scalar=1.0,
-                in1=bias1[:, h],
+                in1=bias1[:, HALF * h : HALF * (h + 1)],
                 op0=ALU.mult,
                 op1=ALU.add,
                 accum_out=live["sums", i][:, h : h + 1],
@@ -207,7 +218,7 @@ def tile_multiheadedattention_pa_w4_kernel(
             ssq = small.tile([P, 1], F32, tag="ssq")
             live["ssq", i] = ssq
             nc.scalar.activation(
-                out=waste[:], in_=live["v", i][:].rearrange("p g t m -> p (g t m)"), func=ACT.Square, bias=live["nmean", i][:],
+                out=waste[:], in_=live["v", i][:], func=ACT.Square, bias=live["nmean", i][:],
                 scale=1.0, accum_out=ssq[:],
             )
 
@@ -215,10 +226,6 @@ def tile_multiheadedattention_pa_w4_kernel(
             r = small.tile([P, 1], F32, tag="r1")
             live["r1", i] = r
             nc.scalar.activation(out=r[:], in_=live.pop(("ssq", i))[:], func=ACT.Abs_reciprocal_sqrt, bias=eps[:], scale=1.0 / D2)
-            if i in Y_ON_SCALAR:
-                nmr = small.tile([P, 1], F32, tag="nmr")
-                live["nmr", i] = nmr
-                nc.scalar.activation(out=nmr[:], in_=live["nmean", i][:], func=ACT.Copy, scale=r[:])
 
         def stage_y(i):
             y = work.tile([P, PASSES2, PACK, P], F32, align_bytes=64, tag="y")
@@ -226,10 +233,10 @@ def tile_multiheadedattention_pa_w4_kernel(
             v = live.pop(("v", i))
             r = live.pop(("r1", i))
             nmean = live.pop(("nmean", i))
-            if i in Y_ON_SCALAR:
-                nc.scalar.activation(out=y[:], in_=v[:], func=ACT.Identity, bias=live.pop(("nmr", i))[:], scale=r[:])
-            else:
-                nc.vector.tensor_scalar(out=y[:], in0=v[:], scalar1=nmean[:], scalar2=r[:], op0=ALU.add, op1=ALU.mult)
+            nc.vector.tensor_scalar(
+                out=y[:].rearrange("p g t m -> p g m t"), in0=v[:].rearrange("p (g m t) -> p g m t", g=PASSES2, t=PACK),
+                scalar1=nmean[:], scalar2=r[:], op0=ALU.add, op1=ALU.mult,
+            )
 
         def turn_y(i, g):
             yt = psum.tile([P, PACK, P], F32, tag="yt")
@@ -250,7 +257,10 @@ def tile_multiheadedattention_pa_w4_kernel(
         def interleave(i, g):
             if ("jg", i) not in live:
                 live["jg", i] = work.tile([P, PASSES2, P, PACK], BF16, align_bytes=64, tag="jg", name="jg")
-            nc.scalar.copy(out=live["jg", i][:, g], in_=live["jp", i][:, g].rearrange("p t r -> p r t"))
+            nc.scalar.copy(
+                out=live["jg", i][:, g].rearrange("p (c i) t -> p c t i", i=4),
+                in_=live["jp", i][:, g].rearrange("p t (c i) -> p c t i", i=4),
+            )
 
         def stage_qj(i):
             jg = live.pop(("jg", i))
@@ -336,7 +346,3 @@ def tile_multiheadedattention_pa_w4_kernel(
             for name, lag in ORDER:
                 if 0 <= step - lag < N_TILES:
                     stages[name](step - lag)
-                    if name == "ex1" and step == lag:
-                        nc.scalar.copy(out=bias1[:], in_=bias1_raw[:].rearrange("p g m t -> p g t m"))
-                        nc.scalar.copy(out=gain1[:], in_=gain1_raw[:])
-                        nc.scalar.copy(out=shift1[:], in_=shift1_raw[:])

@@ -11,6 +11,7 @@ N_TILES = TOKENS // P
 PASSES1 = D // K_PASS
 PASSES2 = D2 // K_PASS
 HALF = 512
+LAST = N_TILES - 1
 EPS = 1e-5
 
 FLOPS = 2 * TOKENS * (D * D2 + D2 * D4)
@@ -27,36 +28,35 @@ ACT = mybir.ActivationFunctionType
 ALU = mybir.AluOpType
 
 ORDER = (
-    ("TT", 0),
-    ("m1", 3),
-    ("in1", 5),
-    ("ty1", 4),
-    ("l2", 8),
-    ("qx", 1),
-    ("b1", 2),
-    ("b0", 2),
-    ("sq", 3),
-    ("tx0", 0),
-    ("re0", 4),
-    ("tx1", 0),
-    ("r2", 15),
-    ("qj", 7),
-    ("r1", 3),
-    ("in0", 4),
-    ("st", 22),
-    ("y", 3),
-    ("l1", 1),
-    ("o1", 14),
-    ("c", 8),
+    ("re0", 6),
+    ("re1", 6),
+    ("y", 4),
+    ("ex0", 1),
     ("rl", 19),
-    ("ty0", 3),
-    ("re1", 4),
-    ("ex0", 0),
-    ("m2", 9),
-    ("l0", 1),
-    ("sq2", 11),
-    ("ex1", 0),
-    ("o2", 16),
+    ("tx1", 1),
+    ("l0", 2),
+    ("st", 19),
+    ("TT", 0),
+    ("sq2", 13),
+    ("m1", 3),
+    ("l2", 10),
+    ("ex1", 1),
+    ("ty0", 5),
+    ("o1", 15),
+    ("qx", 1),
+    ("b0", 2),
+    ("o2", 17),
+    ("r2", 14),
+    ("ty1", 5),
+    ("l1", 2),
+    ("b1", 2),
+    ("sq", 3),
+    ("c", 10),
+    ("in", 6),
+    ("m2", 12),
+    ("r1", 3),
+    ("qj", 8),
+    ("tx0", 0),
 )
 
 
@@ -93,17 +93,20 @@ def tile_multiheadedattention_pa_w4_kernel(
         warm_out = keep.tile([P, 1], F32)
         junk = keep.tile([P, 2], F32)
         ident = keep.tile([P, P], F32, align_bytes=64)
-        scale_rows = keep.tile([P, P], F32, align_bytes=64)
-        scale_cols = keep.tile([P, D // P], F32, align_bytes=64)
+        scale_cols = keep.tile([P, PASSES1, 1, 2, 2], F32, align_bytes=64)
 
-        nc.vector.memset(scale_rows[:], 0.0)
         nc.vector.memset(eps[:], EPS)
         nc.vector.memset(w1_scales[:].rearrange("p g n -> p (g n)").bitcast(I32), 0)
         nc.vector.memset(w2_scales[:].rearrange("p g n -> p (g n)").bitcast(I32), 0)
         make_identity(nc, ident[:])
 
         nc.sync.dma_start(out=x_bytes[:, 0, :], in_=x_hbm[:, 0, :])
-        nc.scalar.dma_start(out=scale_rows[: D // P, :], in_=scale_hbm.rearrange("(c n) -> c n", n=P))
+        nc.scalar.dma_start(
+            out=scale_cols[:].rearrange("p g o u e -> p g (o u e)"), in_=scale_hbm.rearrange("(g p t) -> p g t", p=P, t=PACK)
+        )
+        for g in range(PASSES1):
+            cols = slice(g * K_PASS, (g + 1) * K_PASS)
+            nc.scalar.dma_start(out=x_scale[:, cols], in_=scale_hbm[cols].partition_broadcast(P))
         nc.scalar.activation(out=warm_out[:], in_=eps[:], func=ACT.Abs_reciprocal_sqrt)
         nc.sync.dma_start(out=x_bytes[:, 1, :], in_=x_hbm[:, 1, :])
         for q in range(4):
@@ -132,29 +135,16 @@ def tile_multiheadedattention_pa_w4_kernel(
         nc.gpsimd.tensor_copy(out=gain1[:], in_=gain1_raw[:])
         nc.gpsimd.tensor_copy(out=shift1[:], in_=shift1_raw[:])
 
-        turned = psum.tile([P, P], F32, tag="w", bufs=1)
-        nc.tensor.transpose(turned[:], scale_rows[:], ident[:])
-        nc.vector.tensor_copy(out=scale_cols[:], in_=turned[:, : D // P])
-        for g in range(PASSES1):
-            spread = psum.tile([P, PACK, P], F32, tag=("xt", "yt")[g % 2])
-            for t in range(PACK):
-                nc.tensor.transpose(spread[:, t, :], scale_cols[:, PACK * g + t : PACK * g + t + 1].to_broadcast([P, P]), ident[:])
-            cols = slice(g * K_PASS, (g + 1) * K_PASS)
-            nc.scalar.copy(out=x_scale[:, cols], in_=spread[:].rearrange("p t n -> p (t n)"))
-
         live = {}
 
         def stage_TT(i):
             xs = work.tile([P, D], BF16, align_bytes=64, tag="xs")
             live["xs", i] = xs
-            step = D if i else HALF
-            for c in range(0, D, step):
-                nc.vector.tensor_tensor(
-                    out=xs[:, c : c + step],
-                    in0=x_bytes[:, i, c : c + step].bitcast(F8),
-                    in1=x_scale[:, c : c + step],
-                    op=ALU.mult,
-                )
+            if i == 0:
+                for c in range(0, D, D // 2):
+                    nc.vector.tensor_copy(out=xs[:, c : c + D // 2], in_=x_bytes[:, i, c : c + D // 2].bitcast(F8))
+            else:
+                nc.vector.tensor_tensor(out=xs[:], in0=x_bytes[:, i, :].bitcast(F8), in1=x_scale[:], op=ALU.mult)
 
         def turn_x(i, h):
             words = live["xs", i][:].bitcast(F32)
@@ -168,6 +158,16 @@ def tile_multiheadedattention_pa_w4_kernel(
         def empty_x(i, h):
             if ("xg", i) not in live:
                 live["xg", i] = work.tile([P, PASSES1, P, PACK], BF16, align_bytes=64, tag="xg", name="xg")
+            if i == 0:
+                xt = live.pop(("xt", i, h))
+                for g in range(2):
+                    nc.vector.tensor_tensor(
+                        out=live["xg", i][:, 2 * h + g].rearrange("p r (u e) -> p r u e", u=2),
+                        in0=xt[:, g].rearrange("p u r -> p (u r)").bitcast(BF16).rearrange("p (u r e) -> p r u e", u=2, e=2),
+                        in1=scale_cols[:, 2 * h + g].to_broadcast([P, P, 2, 2]),
+                        op=ALU.mult,
+                    )
+                return
             words = live["xg", i][:].rearrange("p g r t -> p (g r t)").bitcast(F32).rearrange("p (g r u) -> p g r u", g=PASSES1, u=2)
             nc.scalar.copy(out=words[:, 2 * h : 2 * h + 2], in_=live.pop(("xt", i, h))[:].rearrange("p g u r -> p g r u"))
 
@@ -228,53 +228,67 @@ def tile_multiheadedattention_pa_w4_kernel(
             nc.scalar.activation(out=r[:], in_=live.pop(("ssq", i))[:], func=ACT.Abs_reciprocal_sqrt, bias=eps[:], scale=1.0 / D2)
 
         def stage_y(i):
-            y = work.tile([P, PASSES2, PACK, P], F32, align_bytes=64, tag="y")
+            y = work.tile([P, PASSES2, PACK, P], F32, align_bytes=64, tag="y", bufs=6)
             live["y", i] = y
             v = live.pop(("v", i))
-            r = live.pop(("r1", i))
-            nmean = live.pop(("nmean", i))
             nc.vector.tensor_scalar(
                 out=y[:].rearrange("p g t m -> p g m t"), in0=v[:].rearrange("p (g m t) -> p g m t", g=PASSES2, t=PACK),
-                scalar1=nmean[:], scalar2=r[:], op0=ALU.add, op1=ALU.mult,
+                scalar1=live["nmean", i][:], scalar2=live["r1", i][:], op0=ALU.add, op1=ALU.mult,
             )
 
-        def turn_y(i, g):
-            yt = psum.tile([P, PACK, P], F32, tag="yt")
-            live["yt", i, g] = yt
-            for t in range(PACK):
-                nc.tensor.transpose(yt[:, t, :], live["y", i][:, g, t, :], ident[:])
+        def turn_y(i, k):
+            yt = psum.tile([P, 2, 2, P], F32, tag="yt")
+            live["yt", i, k] = yt
+            for a in range(2):
+                for b in range(2):
+                    if i < LAST:
+                        source = live["y", i - i % 2 + b][:, i % 2, 2 * k + a, :]
+                    else:
+                        source = live["y", i][:, k, 2 * a + b, :]
+                    nc.tensor.transpose(yt[:, a, b, :], source, ident[:])
 
-        def relu_1(i, g):
+        def relu_1(i, k):
             if ("jp", i) not in live:
-                live["jp", i] = work.tile([P, PASSES2, PACK, P], BF16, align_bytes=64, tag="jp", name="jp")
-            yt = live.pop(("yt", i, g))
-            for t in range(PACK):
+                live["jp", i] = work.tile([P, 2 * PACK * P], BF16, align_bytes=64, tag="jp", name="jp")
+            yt = live.pop(("yt", i, k))
+            width = 2 * P if i < LAST else P
+            for a in range(2 * 2 * P // width):
+                g, t = (i % 2, 2 * k + a) if i < LAST else (k, a)
+                first = 2 * 2 * P * k + width * a
                 nc.scalar.activation(
-                    out=live["jp", i][:, g, t, :], in_=yt[:, t, :], func=ACT.Relu, bias=shift1[:, g, t : t + 1],
-                    scale=gain1[:, g, t : t + 1],
+                    out=live["jp", i][:, first : first + width],
+                    in_=yt[:].rearrange("p a b r -> p (a b r)")[:, width * a : width * (a + 1)],
+                    func=ACT.Relu, bias=shift1[:, g, t : t + 1], scale=gain1[:, g, t : t + 1],
                 )
 
-        def interleave(i, g):
-            if ("jg", i) not in live:
-                live["jg", i] = work.tile([P, PASSES2, P, PACK], BF16, align_bytes=64, tag="jg", name="jg")
-            nc.scalar.copy(
-                out=live["jg", i][:, g].rearrange("p (c i) t -> p c t i", i=4),
-                in_=live["jp", i][:, g].rearrange("p t (c i) -> p c t i", i=4),
-            )
+        def stage_in(i):
+            jg = work.tile([P, 2 * P * PACK], BF16, align_bytes=64, tag="jg")
+            live["jg", i] = jg
+            jp = live.pop(("jp", i))
+            width = 2 * P * PACK if i < LAST else P * PACK
+            for first in range(0, 2 * P * PACK, width):
+                nc.scalar.copy(
+                    out=jg[:, first : first + width].rearrange("p (c i t) -> p c t i", i=4, t=PACK),
+                    in_=jp[:, first : first + width].rearrange("p (t c i) -> p c t i", i=4, t=PACK),
+                )
 
         def stage_qj(i):
             jg = live.pop(("jg", i))
-            codes = work.tile([P, PASSES2 * P], U32, align_bytes=64, tag="jc")
-            scales = work.tile([P, PASSES2 * P], U8, align_bytes=64, tag="jsc")
+            codes = work.tile([P, 2 * P], U32, align_bytes=64, tag="jc", bufs=6)
+            scales = work.tile([P, 2 * P], U8, align_bytes=64, tag="jsc", bufs=6)
             live["jq", i] = (codes, scales)
-            nc.vector.quantize_mx(out=codes[:].bitcast(FP8X4), scales=scales[:], in_=jg[:].rearrange("p g r t -> p (g r t)"))
+            nc.vector.quantize_mx(out=codes[:].bitcast(FP8X4), scales=scales[:], in_=jg[:])
 
         def stage_l2(i):
-            codes, scales = live.pop(("jq", i))
             w = psum.tile([P, D4], F32, tag="w", bufs=1)
             live["w", i] = w
             for g in range(PASSES2):
-                rows = slice(g * P, (g + 1) * P)
+                if i < LAST:
+                    codes, scales = live["jq", i - i % 2 + g]
+                    rows = slice(i % 2 * P, (i % 2 + 1) * P)
+                else:
+                    codes, scales = live["jq", i]
+                    rows = slice(g * P, (g + 1) * P)
                 nc.tensor.matmul_mx(
                     out=w[:],
                     lhsT=codes[:, rows].bitcast(FP8X4),
@@ -338,7 +352,7 @@ def tile_multiheadedattention_pa_w4_kernel(
             "ex1": lambda i: empty_x(i, 1), "qx": stage_qx, "l0": lambda i: layer1(i, 0), "l1": lambda i: layer1(i, 1),
             "b0": lambda i: bias_1(i, 0), "b1": lambda i: bias_1(i, 1), "m1": stage_m1, "sq": stage_sq, "r1": stage_r1, "y": stage_y,
             "ty0": lambda i: turn_y(i, 0), "ty1": lambda i: turn_y(i, 1), "re0": lambda i: relu_1(i, 0), "re1": lambda i: relu_1(i, 1),
-            "in0": lambda i: interleave(i, 0), "in1": lambda i: interleave(i, 1), "qj": stage_qj, "l2": stage_l2, "c": stage_c,
+            "in": stage_in, "qj": stage_qj, "l2": stage_l2, "c": stage_c,
             "m2": stage_m2, "sq2": stage_sq2, "r2": stage_r2, "o1": stage_o1, "o2": stage_o2, "rl": stage_rl, "st": stage_st,
         }
         lags = [lag for name, lag in ORDER]

@@ -28,35 +28,35 @@ ACT = mybir.ActivationFunctionType
 ALU = mybir.AluOpType
 
 ORDER = (
-    ("re0", 6),
-    ("re1", 6),
-    ("y", 4),
-    ("ex0", 1),
-    ("rl", 19),
-    ("tx1", 1),
     ("l0", 2),
-    ("st", 19),
-    ("TT", 0),
-    ("sq2", 13),
-    ("m1", 3),
-    ("l2", 10),
-    ("ex1", 1),
-    ("ty0", 5),
-    ("o1", 15),
-    ("qx", 1),
-    ("b0", 2),
-    ("o2", 17),
-    ("r2", 14),
-    ("ty1", 5),
-    ("l1", 2),
-    ("b1", 2),
-    ("sq", 3),
-    ("c", 10),
     ("in", 6),
     ("m2", 12),
-    ("r1", 3),
+    ("ty0", 5),
+    ("sq2", 13),
+    ("ex0", 1),
+    ("m1", 3),
+    ("TT", 0),
     ("qj", 8),
+    ("ex1", 1),
+    ("r2", 15),
+    ("c", 10),
+    ("ty1", 5),
+    ("sq", 3),
+    ("l1", 2),
     ("tx0", 0),
+    ("qx", 1),
+    ("b0", 2),
+    ("tx1", 0),
+    ("re0", 5),
+    ("re1", 5),
+    ("l2", 9),
+    ("b1", 2),
+    ("o2", 17),
+    ("r1", 3),
+    ("o1", 15),
+    ("st", 20),
+    ("y", 3),
+    ("rl", 19),
 )
 
 
@@ -93,20 +93,21 @@ def tile_multiheadedattention_pa_w4_kernel(
         warm_out = keep.tile([P, 1], F32)
         junk = keep.tile([P, 2], F32)
         ident = keep.tile([P, P], F32, align_bytes=64)
-        scale_cols = keep.tile([P, PASSES1, 1, 2, 2], F32, align_bytes=64)
+        scale_rows = keep.tile([P, P], F32, align_bytes=64)
+        scale_cols = keep.tile([P, D // P], F32, align_bytes=64)
+        vector_rows = keep.tile([P, D2 + 3 * D4], BF16, align_bytes=64)
+        ones = keep.tile([P, P], BF16, align_bytes=64)
 
+        nc.vector.memset(scale_rows[:], 0.0)
         nc.vector.memset(eps[:], EPS)
         nc.vector.memset(w1_scales[:].rearrange("p g n -> p (g n)").bitcast(I32), 0)
         nc.vector.memset(w2_scales[:].rearrange("p g n -> p (g n)").bitcast(I32), 0)
         make_identity(nc, ident[:])
+        nc.vector.memset(vector_rows[:].bitcast(I32), 0)
+        nc.vector.memset(ones[:], 1.0)
 
         nc.sync.dma_start(out=x_bytes[:, 0, :], in_=x_hbm[:, 0, :])
-        nc.scalar.dma_start(
-            out=scale_cols[:].rearrange("p g o u e -> p g (o u e)"), in_=scale_hbm.rearrange("(g p t) -> p g t", p=P, t=PACK)
-        )
-        for g in range(PASSES1):
-            cols = slice(g * K_PASS, (g + 1) * K_PASS)
-            nc.scalar.dma_start(out=x_scale[:, cols], in_=scale_hbm[cols].partition_broadcast(P))
+        nc.scalar.dma_start(out=scale_rows[: D // P, :], in_=scale_hbm.rearrange("(c n) -> c n", n=P))
         nc.scalar.activation(out=warm_out[:], in_=eps[:], func=ACT.Abs_reciprocal_sqrt)
         nc.sync.dma_start(out=x_bytes[:, 1, :], in_=x_hbm[:, 1, :])
         for q in range(4):
@@ -114,37 +115,54 @@ def tile_multiheadedattention_pa_w4_kernel(
                 out=w1_scales[32 * q : 32 * q + 4, :, :].bitcast(I32),
                 in_=A1W_scales[:, 4 * q : 4 * q + 4, :].rearrange("g q n -> q g n").bitcast(I32),
             )
+        for g in range(PASSES1):
+            nc.sync.dma_start(out=w1[:, g, :], in_=A1W_words[g])
+        nc.sync.dma_start(out=x_bytes[:, 2:4, :], in_=x_hbm[:, 2:4, :])
+        first = 0
+        for vector, width in ((A1b, D2), (A2b, D4), (g2, D4), (b2, D4)):
+            nc.scalar.dma_start(out=vector_rows[0:1, first : first + width], in_=vector.rearrange("(o n) -> o n", o=1))
+            first += width
+        nc.scalar.dma_start(out=gain1_raw[:], in_=g1.rearrange("(g p t) -> p g t", p=P, t=PACK))
+        nc.scalar.dma_start(out=shift1_raw[:], in_=b1.rearrange("(g p t) -> p g t", p=P, t=PACK))
         for q in range(4):
             nc.sync.dma_start(
                 out=w2_scales[32 * q : 32 * q + 4, :, :].bitcast(I32),
                 in_=A2W_scales[:, 4 * q : 4 * q + 4, :].rearrange("g q n -> q g n").bitcast(I32),
             )
-        for g in range(PASSES1):
-            nc.sync.dma_start(out=w1[:, g, :], in_=A1W_words[g])
-        nc.sync.dma_start(out=x_bytes[:, 2:4, :], in_=x_hbm[:, 2:4, :])
-        nc.scalar.dma_start(out=bias1[:], in_=A1b.partition_broadcast(P))
-        nc.scalar.dma_start(out=gain1_raw[:], in_=g1.rearrange("(g p t) -> p g t", p=P, t=PACK))
-        nc.scalar.dma_start(out=shift1_raw[:], in_=b1.rearrange("(g p t) -> p g t", p=P, t=PACK))
         for g in range(PASSES2):
             nc.sync.dma_start(out=w2[:, g, :], in_=A2W_words[g])
-        nc.scalar.dma_start(out=bias2[:], in_=A2b.partition_broadcast(P))
-        nc.scalar.dma_start(out=gain2[:], in_=g2.partition_broadcast(P))
-        nc.scalar.dma_start(out=shift2[:], in_=b2.partition_broadcast(P))
         for first, last in ((4, 8), (8, 12), (12, 17)):
             nc.sync.dma_start(out=x_bytes[:, first:last, :], in_=x_hbm[:, first:last, :])
         nc.gpsimd.tensor_copy(out=gain1[:], in_=gain1_raw[:])
         nc.gpsimd.tensor_copy(out=shift1[:], in_=shift1_raw[:])
+
+        turned = psum.tile([P, P], F32, tag="w")
+        nc.tensor.transpose(turned[:], scale_rows[:], ident[:])
+        nc.vector.tensor_copy(out=scale_cols[:], in_=turned[:, : D // P])
+        for g in range(PASSES1):
+            spread = psum.tile([P, PACK, P], F32, tag=("xt", "yt")[g % 2])
+            for t in range(PACK):
+                nc.tensor.transpose(spread[:, t, :], scale_cols[:, PACK * g + t : PACK * g + t + 1].to_broadcast([P, P]), ident[:])
+            nc.scalar.copy(out=x_scale[:, g * K_PASS : (g + 1) * K_PASS], in_=spread[:].rearrange("p t n -> p (t n)"))
+
+        def spread_vector(target, first, tag):
+            rows = psum.tile([P, HALF], F32, tag=tag)
+            nc.tensor.matmul(out=rows[:], lhsT=ones[:], rhs=vector_rows[:, first : first + HALF], start=True, stop=True)
+            nc.scalar.copy(out=target, in_=rows[:])
 
         live = {}
 
         def stage_TT(i):
             xs = work.tile([P, D], BF16, align_bytes=64, tag="xs")
             live["xs", i] = xs
-            if i == 0:
-                for c in range(0, D, D // 2):
-                    nc.vector.tensor_copy(out=xs[:, c : c + D // 2], in_=x_bytes[:, i, c : c + D // 2].bitcast(F8))
-            else:
-                nc.vector.tensor_tensor(out=xs[:], in0=x_bytes[:, i, :].bitcast(F8), in1=x_scale[:], op=ALU.mult)
+            step = D if i else K_PASS
+            for c in range(0, D, step):
+                nc.vector.tensor_tensor(
+                    out=xs[:, c : c + step],
+                    in0=x_bytes[:, i, c : c + step].bitcast(F8),
+                    in1=x_scale[:, c : c + step],
+                    op=ALU.mult,
+                )
 
         def turn_x(i, h):
             words = live["xs", i][:].bitcast(F32)
@@ -158,16 +176,6 @@ def tile_multiheadedattention_pa_w4_kernel(
         def empty_x(i, h):
             if ("xg", i) not in live:
                 live["xg", i] = work.tile([P, PASSES1, P, PACK], BF16, align_bytes=64, tag="xg", name="xg")
-            if i == 0:
-                xt = live.pop(("xt", i, h))
-                for g in range(2):
-                    nc.vector.tensor_tensor(
-                        out=live["xg", i][:, 2 * h + g].rearrange("p r (u e) -> p r u e", u=2),
-                        in0=xt[:, g].rearrange("p u r -> p (u r)").bitcast(BF16).rearrange("p (u r e) -> p r u e", u=2, e=2),
-                        in1=scale_cols[:, 2 * h + g].to_broadcast([P, P, 2, 2]),
-                        op=ALU.mult,
-                    )
-                return
             words = live["xg", i][:].rearrange("p g r t -> p (g r t)").bitcast(F32).rearrange("p (g r u) -> p g r u", g=PASSES1, u=2)
             nc.scalar.copy(out=words[:, 2 * h : 2 * h + 2], in_=live.pop(("xt", i, h))[:].rearrange("p g u r -> p g r u"))
 
@@ -280,7 +288,7 @@ def tile_multiheadedattention_pa_w4_kernel(
             nc.vector.quantize_mx(out=codes[:].bitcast(FP8X4), scales=scales[:], in_=jg[:])
 
         def stage_l2(i):
-            w = psum.tile([P, D4], F32, tag="w", bufs=1)
+            w = psum.tile([P, D4], F32, tag="w")
             live["w", i] = w
             for g in range(PASSES2):
                 if i < LAST:
@@ -360,3 +368,10 @@ def tile_multiheadedattention_pa_w4_kernel(
             for name, lag in ORDER:
                 if 0 <= step - lag < N_TILES:
                     stages[name](step - lag)
+                    if name == "ex1" and step == lag:
+                        spread_vector(bias1[:, :HALF], 0, "w")
+                        spread_vector(bias1[:, HALF:], HALF, "w")
+                    if name == "ex1" and step == lag + 2:
+                        spread_vector(bias2[:], D2, "w")
+                        spread_vector(gain2[:], D2 + D4, "w")
+                        spread_vector(shift2[:], D2 + 2 * D4, "w")

from contextlib import ExitStack

import concourse.mybir as mybir
from concourse.masks import make_identity

TOKENS, D, D2, D4 = 2176, 2048, 1024, 512
P = 128
PACK = 4
K_PASS = P * PACK
N_TILES = TOKENS // P
PASSES1 = D // K_PASS
PASSES2 = D2 // K_PASS
HALF = 512
LAST = N_TILES - 1
EPS = 1e-5

FLOPS = 2 * TOKENS * (D * D2 + D2 * D4)

F32 = mybir.dt.float32
BF16 = mybir.dt.bfloat16
I32 = mybir.dt.int32
U32 = mybir.dt.uint32
U8 = mybir.dt.uint8
F8 = mybir.dt.float8_e4m3fn
FP8X4 = mybir.dt.float8_e4m3fn_x4
FP4X4 = mybir.dt.float4_e2m1fn_x4
ACT = mybir.ActivationFunctionType
ALU = mybir.AluOpType

ORDER = (
    ("l0", 2),
    ("in", 6),
    ("m2", 12),
    ("ty0", 5),
    ("sq2", 13),
    ("ex0", 1),
    ("m1", 3),
    ("TT", 0),
    ("qj", 8),
    ("ex1", 1),
    ("r2", 15),
    ("c", 10),
    ("ty1", 5),
    ("sq", 3),
    ("l1", 2),
    ("tx0", 0),
    ("qx", 1),
    ("b0", 2),
    ("tx1", 0),
    ("re0", 5),
    ("re1", 5),
    ("l2", 9),
    ("b1", 2),
    ("o2", 17),
    ("r1", 3),
    ("o1", 15),
    ("st", 20),
    ("y", 3),
    ("rl", 19),
)


def tile_multiheadedattention_pa_w4_kernel(
    tc, query_bytes, query_scale, A1W_words, A1W_scales, A1b, g1, b1, A2W_words, A2W_scales, A2b, g2, b2, out
):
    nc = tc.nc
    x_hbm = query_bytes.rearrange("b n k -> (b n) k").rearrange("(i p) k -> p i k", p=P)
    out_hbm = out.rearrange("b n c -> (b n) c").rearrange("(i p) c -> p i c", p=P)
    scale_hbm = query_scale.rearrange("a b k -> (a b k)")

    with ExitStack() as ctx:
        keep = ctx.enter_context(tc.tile_pool(name="keep", bufs=1))
        work = ctx.enter_context(tc.tile_pool(name="work", bufs=4))
        small = ctx.enter_context(tc.tile_pool(name="small", bufs=N_TILES))
        psum = ctx.enter_context(tc.psum_pool(name="psum", bufs=2))
        ctx.enter_context(tc.manual_schedule())

        x_bytes = keep.tile([P, N_TILES, D], U8, align_bytes=64)
        x_scale = keep.tile([P, D], F32, align_bytes=64)
        w1 = keep.tile([P, PASSES1, 2 * D2], U8, align_bytes=64)
        w1_scales = keep.tile([P, PASSES1, D2], U8, align_bytes=64)
        w2 = keep.tile([P, PASSES2, 2 * D4], U8, align_bytes=64)
        w2_scales = keep.tile([P, PASSES2, D4], U8, align_bytes=64)
        bias1 = keep.tile([P, D2], BF16, align_bytes=64)
        bias2 = keep.tile([P, D4], BF16, align_bytes=64)
        gain2 = keep.tile([P, D4], BF16, align_bytes=64)
        shift2 = keep.tile([P, D4], BF16, align_bytes=64)
        gain1_raw = keep.tile([P, PASSES2, PACK], BF16)
        shift1_raw = keep.tile([P, PASSES2, PACK], BF16)
        gain1 = keep.tile([P, PASSES2, PACK], F32)
        shift1 = keep.tile([P, PASSES2, PACK], F32)
        eps = keep.tile([P, 1], F32)
        warm_out = keep.tile([P, 1], F32)
        junk = keep.tile([P, 2], F32)
        ident = keep.tile([P, P], F32, align_bytes=64)
        scale_rows = keep.tile([P, P], F32, align_bytes=64)
        scale_cols = keep.tile([P, D // P], F32, align_bytes=64)
        vector_rows = keep.tile([P, D2 + 3 * D4], BF16, align_bytes=64)
        ones = keep.tile([P, P], BF16, align_bytes=64)

        nc.vector.memset(scale_rows[:], 0.0)
        nc.vector.memset(eps[:], EPS)
        nc.vector.memset(w1_scales[:].rearrange("p g n -> p (g n)").bitcast(I32), 0)
        nc.vector.memset(w2_scales[:].rearrange("p g n -> p (g n)").bitcast(I32), 0)
        make_identity(nc, ident[:])
        nc.vector.memset(vector_rows[:].bitcast(I32), 0)
        nc.vector.memset(ones[:], 1.0)

        nc.sync.dma_start(out=x_bytes[:, 0, :], in_=x_hbm[:, 0, :])
        nc.scalar.dma_start(out=scale_rows[: D // P, :], in_=scale_hbm.rearrange("(c n) -> c n", n=P))
        nc.scalar.activation(out=warm_out[:], in_=eps[:], func=ACT.Abs_reciprocal_sqrt)
        nc.sync.dma_start(out=x_bytes[:, 1, :], in_=x_hbm[:, 1, :])
        for q in range(4):
            nc.sync.dma_start(
                out=w1_scales[32 * q : 32 * q + 4, :, :].bitcast(I32),
                in_=A1W_scales[:, 4 * q : 4 * q + 4, :].rearrange("g q n -> q g n").bitcast(I32),
            )
        for g in range(PASSES1):
            nc.sync.dma_start(out=w1[:, g, :], in_=A1W_words[g])
        nc.sync.dma_start(out=x_bytes[:, 2:4, :], in_=x_hbm[:, 2:4, :])
        first = 0
        for vector, width in ((A1b, D2), (A2b, D4), (g2, D4), (b2, D4)):
            nc.scalar.dma_start(out=vector_rows[0:1, first : first + width], in_=vector.rearrange("(o n) -> o n", o=1))
            first += width
        nc.scalar.dma_start(out=gain1_raw[:], in_=g1.rearrange("(g p t) -> p g t", p=P, t=PACK))
        nc.scalar.dma_start(out=shift1_raw[:], in_=b1.rearrange("(g p t) -> p g t", p=P, t=PACK))
        for q in range(4):
            nc.sync.dma_start(
                out=w2_scales[32 * q : 32 * q + 4, :, :].bitcast(I32),
                in_=A2W_scales[:, 4 * q : 4 * q + 4, :].rearrange("g q n -> q g n").bitcast(I32),
            )
        for g in range(PASSES2):
            nc.sync.dma_start(out=w2[:, g, :], in_=A2W_words[g])
        for first, last in ((4, 8), (8, 12), (12, 17)):
            nc.sync.dma_start(out=x_bytes[:, first:last, :], in_=x_hbm[:, first:last, :])
        nc.gpsimd.tensor_copy(out=gain1[:], in_=gain1_raw[:])
        nc.gpsimd.tensor_copy(out=shift1[:], in_=shift1_raw[:])

        turned = psum.tile([P, P], F32, tag="w")
        nc.tensor.transpose(turned[:], scale_rows[:], ident[:])
        nc.vector.tensor_copy(out=scale_cols[:], in_=turned[:, : D // P])
        for g in range(PASSES1):
            spread = psum.tile([P, PACK, P], F32, tag=("xt", "yt")[g % 2])
            for t in range(PACK):
                nc.tensor.transpose(spread[:, t, :], scale_cols[:, PACK * g + t : PACK * g + t + 1].to_broadcast([P, P]), ident[:])
            nc.scalar.copy(out=x_scale[:, g * K_PASS : (g + 1) * K_PASS], in_=spread[:].rearrange("p t n -> p (t n)"))

        def spread_vector(target, first, tag):
            rows = psum.tile([P, HALF], F32, tag=tag)
            nc.tensor.matmul(out=rows[:], lhsT=ones[:], rhs=vector_rows[:, first : first + HALF], start=True, stop=True)
            nc.scalar.copy(out=target, in_=rows[:])

        live = {}

        def stage_TT(i):
            xs = work.tile([P, D], BF16, align_bytes=64, tag="xs")
            live["xs", i] = xs
            step = D if i else K_PASS
            for c in range(0, D, step):
                nc.vector.tensor_tensor(
                    out=xs[:, c : c + step],
                    in0=x_bytes[:, i, c : c + step].bitcast(F8),
                    in1=x_scale[:, c : c + step],
                    op=ALU.mult,
                )

        def turn_x(i, h):
            words = live["xs", i][:].bitcast(F32)
            xt = psum.tile([P, 2, 2, P], F32, tag="xt")
            live["xt", i, h] = xt
            for g in range(2):
                for u in range(2):
                    first = 256 * (2 * h + g) + u
                    nc.tensor.transpose(xt[:, g, u, :], words[:, first : first - u + 256 : 2], ident[:])

        def empty_x(i, h):
            if ("xg", i) not in live:
                live["xg", i] = work.tile([P, PASSES1, P, PACK], BF16, align_bytes=64, tag="xg", name="xg")
            words = live["xg", i][:].rearrange("p g r t -> p (g r t)").bitcast(F32).rearrange("p (g r u) -> p g r u", g=PASSES1, u=2)
            nc.scalar.copy(out=words[:, 2 * h : 2 * h + 2], in_=live.pop(("xt", i, h))[:].rearrange("p g u r -> p g r u"))

        def stage_qx(i):
            xg = live.pop(("xg", i))
            codes = work.tile([P, PASSES1 * P], U32, align_bytes=64, tag="xc")
            scales = work.tile([P, PASSES1 * P], U8, align_bytes=64, tag="xsc")
            live["xq", i] = (codes, scales)
            nc.vector.quantize_mx(out=codes[:].bitcast(FP8X4), scales=scales[:], in_=xg[:].rearrange("p g r t -> p (g r t)"))

        def layer1(i, h):
            codes, scales = live["xq", i]
            u = psum.tile([P, HALF], F32, tag="u")
            live["u", i, h] = u
            for g in range(PASSES1):
                rows = slice(g * P, (g + 1) * P)
                nc.tensor.matmul_mx(
                    out=u[:],
                    lhsT=codes[:, rows].bitcast(FP8X4),
                    lhsT_scale=scales[:, rows],
                    rhs=w1[:, g, 2 * HALF * h : 2 * HALF * (h + 1)].bitcast(FP4X4),
                    rhs_scale=w1_scales[:, g, HALF * h : HALF * (h + 1)],
                    start=(g == 0),
                    stop=(g == PASSES1 - 1),
                )

        def bias_1(i, h):
            if ("v", i) not in live:
                live["v", i] = work.tile([P, D2], F32, align_bytes=64, tag="v", name="v")
                live["sums", i] = small.tile([P, 2], F32, tag="sums", name="sums")
            nc.vector.scalar_tensor_tensor(
                out=live["v", i][:, HALF * h : HALF * (h + 1)],
                in0=live.pop(("u", i, h))[:],
                scalar=1.0,
                in1=bias1[:, HALF * h : HALF * (h + 1)],
                op0=ALU.mult,
                op1=ALU.add,
                accum_out=live["sums", i][:, h : h + 1],
            )

        def stage_m1(i):
            nmean = small.tile([P, 1], F32, tag="nmean")
            live["nmean", i] = nmean
            nc.scalar.activation(out=junk[:], in_=live.pop(("sums", i))[:], func=ACT.Copy, scale=-1.0 / D2, accum_out=nmean[:])

        def stage_sq(i):
            waste = work.tile([P, D2], BF16, align_bytes=64, tag="waste", bufs=2)
            ssq = small.tile([P, 1], F32, tag="ssq")
            live["ssq", i] = ssq
            nc.scalar.activation(
                out=waste[:], in_=live["v", i][:], func=ACT.Square, bias=live["nmean", i][:],
                scale=1.0, accum_out=ssq[:],
            )

        def stage_r1(i):
            r = small.tile([P, 1], F32, tag="r1")
            live["r1", i] = r
            nc.scalar.activation(out=r[:], in_=live.pop(("ssq", i))[:], func=ACT.Abs_reciprocal_sqrt, bias=eps[:], scale=1.0 / D2)

        def stage_y(i):
            y = work.tile([P, PASSES2, PACK, P], F32, align_bytes=64, tag="y", bufs=6)
            live["y", i] = y
            v = live.pop(("v", i))
            nc.vector.tensor_scalar(
                out=y[:].rearrange("p g t m -> p g m t"), in0=v[:].rearrange("p (g m t) -> p g m t", g=PASSES2, t=PACK),
                scalar1=live["nmean", i][:], scalar2=live["r1", i][:], op0=ALU.add, op1=ALU.mult,
            )

        def turn_y(i, k):
            yt = psum.tile([P, 2, 2, P], F32, tag="yt")
            live["yt", i, k] = yt
            for a in range(2):
                for b in range(2):
                    if i < LAST:
                        source = live["y", i - i % 2 + b][:, i % 2, 2 * k + a, :]
                    else:
                        source = live["y", i][:, k, 2 * a + b, :]
                    nc.tensor.transpose(yt[:, a, b, :], source, ident[:])

        def relu_1(i, k):
            if ("jp", i) not in live:
                live["jp", i] = work.tile([P, 2 * PACK * P], BF16, align_bytes=64, tag="jp", name="jp")
            yt = live.pop(("yt", i, k))
            width = 2 * P if i < LAST else P
            for a in range(2 * 2 * P // width):
                g, t = (i % 2, 2 * k + a) if i < LAST else (k, a)
                first = 2 * 2 * P * k + width * a
                nc.scalar.activation(
                    out=live["jp", i][:, first : first + width],
                    in_=yt[:].rearrange("p a b r -> p (a b r)")[:, width * a : width * (a + 1)],
                    func=ACT.Relu, bias=shift1[:, g, t : t + 1], scale=gain1[:, g, t : t + 1],
                )

        def stage_in(i):
            jg = work.tile([P, 2 * P * PACK], BF16, align_bytes=64, tag="jg")
            live["jg", i] = jg
            jp = live.pop(("jp", i))
            width = 2 * P * PACK if i < LAST else P * PACK
            for first in range(0, 2 * P * PACK, width):
                nc.scalar.copy(
                    out=jg[:, first : first + width].rearrange("p (c i t) -> p c t i", i=4, t=PACK),
                    in_=jp[:, first : first + width].rearrange("p (t c i) -> p c t i", i=4, t=PACK),
                )

        def stage_qj(i):
            jg = live.pop(("jg", i))
            codes = work.tile([P, 2 * P], U32, align_bytes=64, tag="jc", bufs=6)
            scales = work.tile([P, 2 * P], U8, align_bytes=64, tag="jsc", bufs=6)
            live["jq", i] = (codes, scales)
            nc.vector.quantize_mx(out=codes[:].bitcast(FP8X4), scales=scales[:], in_=jg[:])

        def stage_l2(i):
            w = psum.tile([P, D4], F32, tag="w")
            live["w", i] = w
            for g in range(PASSES2):
                if i < LAST:
                    codes, scales = live["jq", i - i % 2 + g]
                    rows = slice(i % 2 * P, (i % 2 + 1) * P)
                else:
                    codes, scales = live["jq", i]
                    rows = slice(g * P, (g + 1) * P)
                nc.tensor.matmul_mx(
                    out=w[:],
                    lhsT=codes[:, rows].bitcast(FP8X4),
                    lhsT_scale=scales[:, rows],
                    rhs=w2[:, g, :].bitcast(FP4X4),
                    rhs_scale=w2_scales[:, g, :],
                    start=(g == 0),
                    stop=(g == PASSES2 - 1),
                )

        def stage_c(i):
            v = work.tile([P, D4], F32, align_bytes=64, tag="v2", bufs=10)
            sums = small.tile([P, 1], F32, tag="sums2")
            live["v2", i] = v
            live["sums2", i] = sums
            nc.vector.scalar_tensor_tensor(
                out=v[:], in0=live.pop(("w", i))[:], scalar=1.0, in1=bias2[:], op0=ALU.mult, op1=ALU.add, accum_out=sums[:]
            )

        def stage_m2(i):
            nmean = small.tile([P, 1], F32, tag="nmean2")
            live["nmean2", i] = nmean
            nc.scalar.activation(out=nmean[:], in_=live.pop(("sums2", i))[:], func=ACT.Copy, scale=-1.0 / D4)

        def stage_sq2(i):
            waste = work.tile([P, D4], BF16, align_bytes=64, tag="waste2", bufs=2)
            ssq = small.tile([P, 1], F32, tag="ssq2")
            live["ssq2", i] = ssq
            nc.scalar.activation(out=waste[:], in_=live["v2", i][:], func=ACT.Square, bias=live["nmean2", i][:], scale=1.0, accum_out=ssq[:])

        def stage_r2(i):
            r = small.tile([P, 1], F32, tag="r2")
            live["r2", i] = r
            nc.scalar.activation(out=r[:], in_=live.pop(("ssq2", i))[:], func=ACT.Abs_reciprocal_sqrt, bias=eps[:], scale=1.0 / D4)

        def stage_o1(i):
            z = work.tile([P, D4], F32, align_bytes=64, tag="z")
            live["z", i] = z
            nc.vector.scalar_tensor_tensor(
                out=z[:], in0=live["v2", i][:], scalar=live["nmean2", i][:], in1=gain2[:], op0=ALU.add, op1=ALU.mult
            )

        def stage_o2(i):
            o = work.tile([P, D4], F32, align_bytes=64, tag="o")
            live["o", i] = o
            nc.vector.scalar_tensor_tensor(
                out=o[:], in0=live.pop(("z", i))[:], scalar=live.pop(("r2", i))[:], in1=shift2[:], op0=ALU.mult, op1=ALU.add
            )

        def stage_rl(i):
            o = live.pop(("o", i))
            res = work.tile([P, D4], F32, align_bytes=64, tag="res")
            live["res", i] = res
            nc.scalar.activation(out=res[:], in_=o[:], func=ACT.Relu)

        def stage_st(i):
            nc.sync.dma_start(out=out_hbm[:, i, :], in_=live.pop(("res", i))[:])

        stages = {
            "TT": stage_TT, "tx0": lambda i: turn_x(i, 0), "tx1": lambda i: turn_x(i, 1), "ex0": lambda i: empty_x(i, 0),
            "ex1": lambda i: empty_x(i, 1), "qx": stage_qx, "l0": lambda i: layer1(i, 0), "l1": lambda i: layer1(i, 1),
            "b0": lambda i: bias_1(i, 0), "b1": lambda i: bias_1(i, 1), "m1": stage_m1, "sq": stage_sq, "r1": stage_r1, "y": stage_y,
            "ty0": lambda i: turn_y(i, 0), "ty1": lambda i: turn_y(i, 1), "re0": lambda i: relu_1(i, 0), "re1": lambda i: relu_1(i, 1),
            "in": stage_in, "qj": stage_qj, "l2": stage_l2, "c": stage_c,
            "m2": stage_m2, "sq2": stage_sq2, "r2": stage_r2, "o1": stage_o1, "o2": stage_o2, "rl": stage_rl, "st": stage_st,
        }
        lags = [lag for name, lag in ORDER]
        for step in range(min(lags), N_TILES + max(lags)):
            for name, lag in ORDER:
                if 0 <= step - lag < N_TILES:
                    stages[name](step - lag)
                    if name == "ex1" and step == lag:
                        spread_vector(bias1[:, :HALF], 0, "w")
                        spread_vector(bias1[:, HALF:], HALF, "w")
                    if name == "ex1" and step == lag + 2:
                        spread_vector(bias2[:], D2, "w")
                        spread_vector(gain2[:], D2 + D4, "w")
                        spread_vector(shift2[:], D2 + 2 * D4, "w")
